import numpy as np
import ml_dtypes


def mxq(x, axis, fmt="e4m3"):
    dtype, down = {"e4m3": (ml_dtypes.float8_e4m3fn, 7), "e5m2": (ml_dtypes.float8_e5m2, 14)}[fmt]
    v = np.moveaxis(np.asarray(x, np.float32).astype(ml_dtypes.bfloat16).astype(np.float64), axis, -1)
    blocks = v.reshape(v.shape[:-1] + (-1, 32))
    amax = np.abs(blocks).max(-1, keepdims=True)
    byte = np.maximum(np.where(amax > 0, np.frexp(amax)[1] - 1 + 127, 0) - down, 1)
    scale = np.exp2(byte - 127.0)
    codes = (blocks / scale).astype(np.float32).astype(dtype).astype(np.float64)
    return np.moveaxis((codes * scale).reshape(v.shape), -1, axis)


WIDE = False


def mx_kscale(k):
    if not WIDE:
        return np.ones(k)
    levels = np.array([20, -20, 10, -10, 0])
    a = np.random.permutation(np.resize(levels, k // 512 * 4)).reshape(k // 512, 4)
    idx = np.arange(k)
    return np.exp2(a[idx // 512, idx % 128 // 32])


BF16 = ml_dtypes.bfloat16


def bf(x):
    return np.asarray(x, np.float32).astype(BF16)


def f64(x):
    return np.asarray(x).astype(np.float64)


B, D, H = 1024, 512, 1024


def sigmoid(v):
    return 1.0 / (1.0 + np.exp(-v))


def setup_inputs():
    u = mx_kscale(H)
    x = bf(np.random.standard_normal((B, D)))
    w0 = bf(np.random.standard_normal((4 * H, D)) * 1.5 / np.sqrt(D))
    b_ih0 = bf(np.random.standard_normal(4 * H) * 0.3)
    b_hh0 = bf(np.random.standard_normal(4 * H) * 0.3)
    g = bf(np.random.standard_normal((B, H)) * np.exp2(np.random.randint(-12, 1, (B, 1))) * 8.0 * u[None, :])
    a = f64(x) @ f64(w0).T + f64(b_ih0) + f64(b_hh0)
    div = np.concatenate([u, np.ones(H), u, u])
    return {"x": x,
            "W_ih0": bf(f64(w0) / div[:, None]),
            "b_ih0": b_ih0,
            "b_hh0": b_hh0,
            "a_i": np.asarray(a[:, :H], np.float32),
            "a_g": np.asarray(a[:, 2 * H:3 * H], np.float32),
            "a_o": np.asarray(a[:, 3 * H:], np.float32),
            "grad_out": g}


def reference(x, W_ih0, b_ih0, b_hh0, a_i, a_g, a_o, grad_out):
    w = f64(W_ih0)
    g = f64(grad_out)
    si = sigmoid(f64(a_i))
    tg = np.tanh(f64(a_g))
    so = sigmoid(f64(a_o))
    tc = np.tanh(si * tg)
    dc = g * so * (1.0 - tc * tc)
    da_i = dc * tg * si * (1.0 - si)
    da_g = dc * si * (1.0 - tg * tg)
    da_o = g * tc * so * (1.0 - so)
    da = np.concatenate([da_i, da_g, da_o], axis=1)
    wu = np.concatenate([w[:H], w[2 * H:]], axis=0)
    return mxq(da, 1, "e5m2") @ mxq(wu, 0, "e4m3")

@@ -1,0 +1,203 @@
+from contextlib import ExitStack
+
+import concourse.mybir as mybir
+from concourse.masks import make_identity
+
+F32 = mybir.dt.float32
+BF16 = mybir.dt.bfloat16
+U32 = mybir.dt.uint32
+U8 = mybir.dt.uint8
+E4M3_X4 = mybir.dt.float8_e4m3fn_x4
+E5M2_X4 = mybir.dt.float8_e5m2_x4
+FUNC = mybir.ActivationFunctionType
+ALU = mybir.AluOpType
+
+P = 128
+PACK = 4
+K_PASS = P * PACK
+B, D, H = 1024, 512, 1024
+BLOCKS = B // P
+HALVES = H // K_PASS
+GATE_ROW = (0, 2 * H, 3 * H)
+PASSES = len(GATE_ROW) * HALVES
+
+FLOPS = 2 * B * 3 * H * D
+BYTES = 3 * B * H * 4 + B * H * 2 + 3 * H * D * 2 + B * D * 4
+
+
+def flat(tile_ap):
+    return tile_ap.rearrange("p h w t -> p (h w t)")
+
+
+def tile_lstmbaseline_pa_v_kernel(tc, x, W_ih0, b_ih0, b_hh0, a_i, a_g, a_o, grad_out, out):
+    nc = tc.nc
+    with ExitStack() as ctx:
+        const = ctx.enter_context(tc.tile_pool(name="const", bufs=1))
+        loads = ctx.enter_context(tc.tile_pool(name="loads", bufs=3))
+        keep3 = ctx.enter_context(tc.tile_pool(name="keep3", bufs=3))
+        work = ctx.enter_context(tc.tile_pool(name="work", bufs=2))
+        mxop = ctx.enter_context(tc.tile_pool(name="mxop", bufs=4))
+        wraw = ctx.enter_context(tc.tile_pool(name="wraw", bufs=PASSES))
+        psum_a = ctx.enter_context(tc.psum_pool(name="psum_a", bufs=2))
+        psum_g = ctx.enter_context(tc.psum_pool(name="psum_g", bufs=1))
+        psum_o = ctx.enter_context(tc.psum_pool(name="psum_o", bufs=1))
+
+        ident_f32 = const.tile([P, P], F32)
+        make_identity(nc, ident_f32[:])
+        ident_bf16 = const.tile([P, P], BF16)
+        make_identity(nc, ident_bf16[:])
+        w_codes = const.tile([P, PASSES, D], U32, align_bytes=64)
+        w_scales = const.tile([P, PASSES, D], U8, align_bytes=64)
+
+        shape_t = [P, HALVES, P, PACK]
+
+        def load_block(r):
+            rows = slice(r * P, (r + 1) * P)
+            ai = loads.tile([P, H], F32)
+            nc.sync.dma_start(out=ai[:], in_=a_i[rows, :])
+            ag = loads.tile([P, H], F32)
+            nc.sync.dma_start(out=ag[:], in_=a_g[rows, :])
+            ao = loads.tile([P, H], F32)
+            nc.sync.dma_start(out=ao[:], in_=a_o[rows, :])
+            go = loads.tile([P, H], BF16)
+            nc.sync.dma_start(out=go[:], in_=grad_out[rows, :])
+            return ai, ag, ao, go
+
+        def load_weights(c):
+            row0 = GATE_ROW[c // HALVES] + (c % HALVES) * K_PASS
+            raw = wraw.tile([P, PACK, D], BF16)
+            nc.sync.dma_start(
+                out=raw[:], in_=W_ih0[row0 : row0 + K_PASS, :].rearrange("(t p) n -> p t n", p=P)
+            )
+            return raw
+
+        def quantise_weights(c, raw):
+            grouped = work.tile([P, D, PACK], BF16, align_bytes=64)
+            nc.scalar.copy(
+                out=grouped[:].rearrange("p (c i) t -> p c t i", i=4),
+                in_=raw[:].rearrange("p t (c i) -> p c t i", i=4),
+            )
+            nc.vector.quantize_mx(
+                out=w_codes[:, c, :].bitcast(E4M3_X4),
+                scales=w_scales[:, c, :],
+                in_=grouped[:].rearrange("p n t -> p (n t)"),
+            )
+
+        def transposed_tanh(src, dst, scale, h, bank):
+            for t in range(PACK):
+                col0 = h * K_PASS + t * P
+                nc.tensor.transpose(bank[:, t, :], src[:, col0 : col0 + P], ident_f32[:])
+            nc.scalar.activation(
+                out=dst[:, h], in_=bank[:].rearrange("p t w -> p w t"), func=FUNC.Tanh, scale=scale
+            )
+
+        def front(block):
+            ai, ag, ao, go = block
+            ti = keep3.tile(shape_t, F32)
+            tg = work.tile(shape_t, F32)
+            to = work.tile(shape_t, F32)
+            g_t = psum_g.tile([P, HALVES, PACK, P], BF16)
+            for h in range(HALVES):
+                ai_t = psum_a.tile([P, PACK, P], F32)
+                transposed_tanh(ai, ti, 0.5, h, ai_t)
+                ag_t = psum_a.tile([P, PACK, P], F32)
+                transposed_tanh(ag, tg, 1.0, h, ag_t)
+                ao_t = psum_a.tile([P, PACK, P], F32)
+                transposed_tanh(ao, to, 0.5, h, ao_t)
+                for t in range(PACK):
+                    col0 = h * K_PASS + t * P
+                    nc.tensor.transpose(g_t[:, h, t, :], go[:, col0 : col0 + P], ident_bf16[:])
+            return ti, tg, to, g_t
+
+        def stage_a(fr):
+            ti, tg, to, g_t = fr
+            u = work.tile(shape_t, F32)
+            nc.vector.scalar_tensor_tensor(
+                out=flat(u[:]), in0=flat(ti[:]), scalar=1.0, in1=flat(tg[:]), op0=ALU.add, op1=ALU.mult
+            )
+            gs = work.tile(shape_t, F32)
+            for h in range(HALVES):
+                nc.vector.scalar_tensor_tensor(
+                    out=gs[:, h], in0=to[:, h], scalar=1.0,
+                    in1=g_t[:, h].rearrange("p t w -> p w t"), op0=ALU.add, op1=ALU.mult,
+                )
+            t1 = work.tile(shape_t, F32)
+            nc.vector.scalar_tensor_tensor(
+                out=flat(t1[:]), in0=flat(to[:]), scalar=-1.0, in1=flat(gs[:]), op0=ALU.add, op1=ALU.mult
+            )
+            tch = work.tile(shape_t, F32)
+            nc.scalar.activation(out=flat(tch[:]), in_=flat(u[:]), func=FUNC.Tanh, scale=0.5)
+            tc2 = work.tile(shape_t, F32)
+            nc.scalar.activation(out=flat(tc2[:]), in_=flat(tch[:]), func=FUNC.Square)
+            tg2q = work.tile(shape_t, F32)
+            nc.scalar.activation(out=flat(tg2q[:]), in_=flat(tg[:]), func=FUNC.Square, scale=0.5)
+            return ti, u, gs, t1, tch, tc2, tg2q
+
+        def quantise(da):
+            codes = mxop.tile([P, HALVES * P], U32, align_bytes=64, name="codes_" + da[0], tag="codes_" + da[0])
+            scales = mxop.tile([P, HALVES * P], U8, align_bytes=64, name="scales_" + da[0], tag="scales_" + da[0])
+            nc.vector.quantize_mx(out=codes[:].bitcast(E5M2_X4), scales=scales[:], in_=flat(da[1][:]))
+            return codes, scales
+
+        def stage_b(st):
+            ti, u, gs, t1, tch, tc2, tg2q = st
+            xx = work.tile(shape_t, F32)
+            nc.vector.scalar_tensor_tensor(
+                out=flat(xx[:]), in0=flat(tc2[:]), scalar=-1.0, in1=flat(gs[:]), op0=ALU.add, op1=ALU.mult
+            )
+            da_o = work.tile(shape_t, BF16, align_bytes=64)
+            nc.vector.scalar_tensor_tensor(
+                out=flat(da_o[:]), in0=flat(t1[:]), scalar=-0.25, in1=flat(tch[:]), op0=ALU.mult, op1=ALU.mult
+            )
+            t2 = work.tile(shape_t, F32)
+            nc.vector.scalar_tensor_tensor(
+                out=flat(t2[:]), in0=flat(xx[:]), scalar=0.125, in1=flat(u[:]), op0=ALU.mult, op1=ALU.mult
+            )
+            t3 = work.tile(shape_t, F32)
+            nc.vector.scalar_tensor_tensor(
+                out=flat(t3[:]), in0=flat(tg2q[:]), scalar=-0.25, in1=flat(xx[:]), op0=ALU.add, op1=ALU.mult
+            )
+            da_i = work.tile(shape_t, BF16, align_bytes=64)
+            nc.vector.scalar_tensor_tensor(
+                out=flat(da_i[:]), in0=flat(ti[:]), scalar=-1.0, in1=flat(t2[:]), op0=ALU.add, op1=ALU.mult
+            )
+            da_g = work.tile(shape_t, BF16, align_bytes=64)
+            nc.vector.scalar_tensor_tensor(
+                out=flat(da_g[:]), in0=flat(ti[:]), scalar=1.0, in1=flat(t3[:]), op0=ALU.add, op1=ALU.mult
+            )
+            return [quantise(("i", da_i)), quantise(("g", da_g)), quantise(("o", da_o))]
+
+        def multiply(r, operands):
+            acc = psum_o.tile([P, D], F32)
+            for c in range(PASSES):
+                codes, scales = operands[c // HALVES]
+                cols = slice((c % HALVES) * P, (c % HALVES + 1) * P)
+                nc.tensor.matmul_mx(
+                    out=acc[:],
+                    lhsT=codes[:, cols].bitcast(E5M2_X4),
+                    lhsT_scale=scales[:, cols],
+                    rhs=w_codes[:, c, :].bitcast(E4M3_X4),
+                    rhs_scale=w_scales[:, c, :],
+                    start=(c == 0),
+                    stop=(c == PASSES - 1),
+                )
+            res = work.tile([P, D], F32)
+            nc.scalar.copy(out=res[:], in_=acc[:])
+            nc.sync.dma_start(out=out[r * P : (r + 1) * P, :], in_=res[:])
+
+        blocks = {0: load_block(0), 1: load_block(1)}
+        raws = [load_weights(c) for c in range(PASSES)]
+        fronts = {0: front(blocks[0])}
+        stages = {}
+        for r in range(BLOCKS):
+            if r + 2 < BLOCKS:
+                blocks[r + 2] = load_block(r + 2)
+            if r + 1 < BLOCKS:
+                fronts[r + 1] = front(blocks[r + 1])
+            stages[r] = stage_a(fronts[r])
+            if r < 2:
+                for c in range(3 * r, 3 * r + 3):
+                    quantise_weights(c, raws[c])
+            if r >= 1:
+                multiply(r - 1, stage_b(stages[r - 1]))
+        multiply(BLOCKS - 1, stage_b(stages[BLOCKS - 1]))

@@ -25,43 +25,23 @@ FLOPS = 2 * B * 3 * H * D
 BYTES = 3 * B * H * 4 + B * H * 2 + 3 * H * D * 2 + B * D * 4
 
 
-def flat(tile_ap):
-    return tile_ap.rearrange("p h w t -> p (h w t)")
-
-
 def tile_lstmbaseline_pa_v_kernel(tc, x, W_ih0, b_ih0, b_hh0, a_i, a_g, a_o, grad_out, out):
     nc = tc.nc
     with ExitStack() as ctx:
         const = ctx.enter_context(tc.tile_pool(name="const", bufs=1))
-        loads = ctx.enter_context(tc.tile_pool(name="loads", bufs=3))
-        keep3 = ctx.enter_context(tc.tile_pool(name="keep3", bufs=3))
-        work = ctx.enter_context(tc.tile_pool(name="work", bufs=2))
-        mxop = ctx.enter_context(tc.tile_pool(name="mxop", bufs=4))
+        rows_pool = ctx.enter_context(tc.tile_pool(name="rows_pool", bufs=3))
+        cols_pool = ctx.enter_context(tc.tile_pool(name="cols_pool", bufs=3))
+        mxop = ctx.enter_context(tc.tile_pool(name="mxop", bufs=3))
         wraw = ctx.enter_context(tc.tile_pool(name="wraw", bufs=PASSES))
-        psum_a = ctx.enter_context(tc.psum_pool(name="psum_a", bufs=2))
-        psum_g = ctx.enter_context(tc.psum_pool(name="psum_g", bufs=1))
+        psum_t = ctx.enter_context(tc.psum_pool(name="psum_t", bufs=1))
         psum_o = ctx.enter_context(tc.psum_pool(name="psum_o", bufs=1))
 
-        ident_f32 = const.tile([P, P], F32)
-        make_identity(nc, ident_f32[:])
-        ident_bf16 = const.tile([P, P], BF16)
-        make_identity(nc, ident_bf16[:])
+        ident = const.tile([P, P], F32)
+        make_identity(nc, ident[:])
+        minus_half = const.tile([P, 1], F32)
+        nc.vector.memset(minus_half[:], -0.5)
         w_codes = const.tile([P, PASSES, D], U32, align_bytes=64)
         w_scales = const.tile([P, PASSES, D], U8, align_bytes=64)
-
-        shape_t = [P, HALVES, P, PACK]
-
-        def load_block(r):
-            rows = slice(r * P, (r + 1) * P)
-            ai = loads.tile([P, H], F32)
-            nc.sync.dma_start(out=ai[:], in_=a_i[rows, :])
-            ag = loads.tile([P, H], F32)
-            nc.sync.dma_start(out=ag[:], in_=a_g[rows, :])
-            ao = loads.tile([P, H], F32)
-            nc.sync.dma_start(out=ao[:], in_=a_o[rows, :])
-            go = loads.tile([P, H], BF16)
-            nc.sync.dma_start(out=go[:], in_=grad_out[rows, :])
-            return ai, ag, ao, go
 
         def load_weights(c):
             row0 = GATE_ROW[c // HALVES] + (c % HALVES) * K_PASS
@@ -72,8 +52,8 @@ def tile_lstmbaseline_pa_v_kernel(tc, x, W_ih0, b_ih0, b_hh0, a_i, a_g, a_o, gra
             return raw
 
         def quantise_weights(c, raw):
-            grouped = work.tile([P, D, PACK], BF16, align_bytes=64)
-            nc.scalar.copy(
+            grouped = cols_pool.tile([P, D, PACK], BF16, align_bytes=64, bufs=2)
+            nc.vector.tensor_copy(
                 out=grouped[:].rearrange("p (c i) t -> p c t i", i=4),
                 in_=raw[:].rearrange("p t (c i) -> p c t i", i=4),
             )
@@ -83,93 +63,86 @@ def tile_lstmbaseline_pa_v_kernel(tc, x, W_ih0, b_ih0, b_hh0, a_i, a_g, a_o, gra
                 in_=grouped[:].rearrange("p n t -> p (n t)"),
             )
 
-        def transposed_tanh(src, dst, scale, h, bank):
+        def load_block(r):
+            rows = slice(r * P, (r + 1) * P)
+            si = rows_pool.tile([P, H], F32, bufs=4)
+            nc.sync.dma_start(out=si[:], in_=a_i[rows, :])
+            tg = rows_pool.tile([P, H], F32)
+            nc.sync.dma_start(out=tg[:], in_=a_g[rows, :])
+            so = rows_pool.tile([P, H], F32, bufs=4)
+            nc.sync.dma_start(out=so[:], in_=a_o[rows, :])
+            go = rows_pool.tile([P, H], BF16, bufs=4)
+            nc.sync.dma_start(out=go[:], in_=grad_out[rows, :])
+            return si, tg, so, go
+
+        def gates(block):
+            si, tg, so, go = block
+            nc.scalar.activation(out=si[:], in_=si[:], func=FUNC.Sigmoid)
+            nc.scalar.activation(out=tg[:], in_=tg[:], func=FUNC.Tanh)
+            nc.scalar.activation(out=so[:], in_=so[:], func=FUNC.Sigmoid)
+            cc = rows_pool.tile([P, H], F32)
+            nc.gpsimd.tensor_tensor(out=cc[:], in0=si[:], in1=tg[:], op=ALU.mult)
+            gso = rows_pool.tile([P, H], F32)
+            nc.gpsimd.tensor_tensor(out=gso[:], in0=so[:], in1=go[:], op=ALU.mult)
+            return si, tg, so, go, cc, gso
+
+        def cell(gt):
+            si, tg, so, go, cc, gso = gt
+            ntc = rows_pool.tile([P, H], F32)
+            nc.scalar.activation(out=ntc[:], in_=cc[:], func=FUNC.Tanh, scale=-1.0)
+            tg2 = rows_pool.tile([P, H], F32)
+            nc.scalar.activation(out=tg2[:], in_=tg[:], func=FUNC.Square)
+            n1 = rows_pool.tile([P, H], F32)
+            nc.gpsimd.tensor_tensor(out=n1[:], in0=ntc[:], in1=go[:], op=ALU.mult)
+            return {"si": si, "so": so, "cc": cc, "gso": gso, "ntc": ntc, "tg2": tg2, "n1": n1}
+
+        def turned(nat, key, h):
+            bank = psum_t.tile([P, PACK, P], F32, name="bank_" + key, tag="bank_" + key)
             for t in range(PACK):
                 col0 = h * K_PASS + t * P
-                nc.tensor.transpose(bank[:, t, :], src[:, col0 : col0 + P], ident_f32[:])
-            nc.scalar.activation(
-                out=dst[:, h], in_=bank[:].rearrange("p t w -> p w t"), func=FUNC.Tanh, scale=scale
-            )
+                nc.tensor.transpose(bank[:, t, :], nat[key][:, col0 : col0 + P], ident[:])
+            return bank[:].rearrange("p t w -> p w t")
 
-        def front(block):
-            ai, ag, ao, go = block
-            ti = keep3.tile(shape_t, F32)
-            tg = work.tile(shape_t, F32)
-            to = work.tile(shape_t, F32)
-            g_t = psum_g.tile([P, HALVES, PACK, P], BF16)
-            for h in range(HALVES):
-                ai_t = psum_a.tile([P, PACK, P], F32)
-                transposed_tanh(ai, ti, 0.5, h, ai_t)
-                ag_t = psum_a.tile([P, PACK, P], F32)
-                transposed_tanh(ag, tg, 1.0, h, ag_t)
-                ao_t = psum_a.tile([P, PACK, P], F32)
-                transposed_tanh(ao, to, 0.5, h, ao_t)
-                for t in range(PACK):
-                    col0 = h * K_PASS + t * P
-                    nc.tensor.transpose(g_t[:, h, t, :], go[:, col0 : col0 + P], ident_bf16[:])
-            return ti, tg, to, g_t
-
-        def stage_a(fr):
-            ti, tg, to, g_t = fr
-            u = work.tile(shape_t, F32)
+        def products(nat, h, da_i, da_g, da_o):
+            so_t = turned(nat, "so", h)
+            sq_o = cols_pool.tile([P, P, PACK], F32)
+            nc.scalar.activation(out=sq_o[:], in_=so_t, func=FUNC.Square, bias=minus_half[:])
+            ntc_t = turned(nat, "ntc", h)
+            tc2 = cols_pool.tile([P, P, PACK], F32)
+            nc.scalar.activation(out=tc2[:], in_=ntc_t, func=FUNC.Square)
+            gso_t = turned(nat, "gso", h)
+            xx = cols_pool.tile([P, P, PACK], F32)
             nc.vector.scalar_tensor_tensor(
-                out=flat(u[:]), in0=flat(ti[:]), scalar=1.0, in1=flat(tg[:]), op0=ALU.add, op1=ALU.mult
+                out=xx[:], in0=tc2[:], scalar=-1.0, in1=gso_t, op0=ALU.add, op1=ALU.mult
             )
-            gs = work.tile(shape_t, F32)
-            for h in range(HALVES):
-                nc.vector.scalar_tensor_tensor(
-                    out=gs[:, h], in0=to[:, h], scalar=1.0,
-                    in1=g_t[:, h].rearrange("p t w -> p w t"), op0=ALU.add, op1=ALU.mult,
-                )
-            t1 = work.tile(shape_t, F32)
+            n1_t = turned(nat, "n1", h)
             nc.vector.scalar_tensor_tensor(
-                out=flat(t1[:]), in0=flat(to[:]), scalar=-1.0, in1=flat(gs[:]), op0=ALU.add, op1=ALU.mult
+                out=da_o[:, h], in0=sq_o[:], scalar=-0.25, in1=n1_t, op0=ALU.add, op1=ALU.mult
             )
-            tch = work.tile(shape_t, F32)
-            nc.scalar.activation(out=flat(tch[:]), in_=flat(u[:]), func=FUNC.Tanh, scale=0.5)
-            tc2 = work.tile(shape_t, F32)
-            nc.scalar.activation(out=flat(tc2[:]), in_=flat(tch[:]), func=FUNC.Square)
-            tg2q = work.tile(shape_t, F32)
-            nc.scalar.activation(out=flat(tg2q[:]), in_=flat(tg[:]), func=FUNC.Square, scale=0.5)
-            return ti, u, gs, t1, tch, tc2, tg2q
+            si_t = turned(nat, "si", h)
+            f1 = cols_pool.tile([P, P, PACK], F32)
+            nc.vector.scalar_tensor_tensor(
+                out=f1[:], in0=si_t, scalar=-1.0, in1=xx[:], op0=ALU.add, op1=ALU.mult
+            )
+            e1 = cols_pool.tile([P, P, PACK], F32)
+            nc.vector.tensor_tensor(out=e1[:], in0=si_t, in1=xx[:], op=ALU.mult)
+            cc_t = turned(nat, "cc", h)
+            nc.vector.tensor_tensor(out=da_i[:, h], in0=cc_t, in1=f1[:], op=ALU.mult)
+            tg2_t = turned(nat, "tg2", h)
+            nc.vector.scalar_tensor_tensor(
+                out=da_g[:, h], in0=tg2_t, scalar=-1.0, in1=e1[:], op0=ALU.add, op1=ALU.mult
+            )
 
-        def quantise(da):
-            codes = mxop.tile([P, HALVES * P], U32, align_bytes=64, name="codes_" + da[0], tag="codes_" + da[0])
-            scales = mxop.tile([P, HALVES * P], U8, align_bytes=64, name="scales_" + da[0], tag="scales_" + da[0])
-            nc.vector.quantize_mx(out=codes[:].bitcast(E5M2_X4), scales=scales[:], in_=flat(da[1][:]))
+        def quantise(key, da):
+            codes = mxop.tile([P, HALVES * P], U32, align_bytes=64, name="codes_" + key, tag="codes_" + key)
+            scales = mxop.tile([P, HALVES * P], U8, align_bytes=64, name="scales_" + key, tag="scales_" + key)
+            nc.vector.quantize_mx(
+                out=codes[:].bitcast(E5M2_X4), scales=scales[:], in_=da[:].rearrange("p h w t -> p (h w t)")
+            )
             return codes, scales
 
-        def stage_b(st):
-            ti, u, gs, t1, tch, tc2, tg2q = st
-            xx = work.tile(shape_t, F32)
-            nc.vector.scalar_tensor_tensor(
-                out=flat(xx[:]), in0=flat(tc2[:]), scalar=-1.0, in1=flat(gs[:]), op0=ALU.add, op1=ALU.mult
-            )
-            da_o = work.tile(shape_t, BF16, align_bytes=64)
-            nc.vector.scalar_tensor_tensor(
-                out=flat(da_o[:]), in0=flat(t1[:]), scalar=-0.25, in1=flat(tch[:]), op0=ALU.mult, op1=ALU.mult
-            )
-            t2 = work.tile(shape_t, F32)
-            nc.vector.scalar_tensor_tensor(
-                out=flat(t2[:]), in0=flat(xx[:]), scalar=0.125, in1=flat(u[:]), op0=ALU.mult, op1=ALU.mult
-            )
-            t3 = work.tile(shape_t, F32)
-            nc.vector.scalar_tensor_tensor(
-                out=flat(t3[:]), in0=flat(tg2q[:]), scalar=-0.25, in1=flat(xx[:]), op0=ALU.add, op1=ALU.mult
-            )
-            da_i = work.tile(shape_t, BF16, align_bytes=64)
-            nc.vector.scalar_tensor_tensor(
-                out=flat(da_i[:]), in0=flat(ti[:]), scalar=-1.0, in1=flat(t2[:]), op0=ALU.add, op1=ALU.mult
-            )
-            da_g = work.tile(shape_t, BF16, align_bytes=64)
-            nc.vector.scalar_tensor_tensor(
-                out=flat(da_g[:]), in0=flat(ti[:]), scalar=1.0, in1=flat(t3[:]), op0=ALU.add, op1=ALU.mult
-            )
-            return [quantise(("i", da_i)), quantise(("g", da_g)), quantise(("o", da_o))]
-
-        def multiply(r, operands):
-            acc = psum_o.tile([P, D], F32)
-            for c in range(PASSES):
+        def multiply(acc, operands, passes):
+            for c in passes:
                 codes, scales = operands[c // HALVES]
                 cols = slice((c % HALVES) * P, (c % HALVES + 1) * P)
                 nc.tensor.matmul_mx(
@@ -181,23 +154,40 @@ def tile_lstmbaseline_pa_v_kernel(tc, x, W_ih0, b_ih0, b_hh0, a_i, a_g, a_o, gra
                     start=(c == 0),
                     stop=(c == PASSES - 1),
                 )
-            res = work.tile([P, D], F32)
+
+        def store(r, acc):
+            res = cols_pool.tile([P, D], F32, bufs=2)
             nc.scalar.copy(out=res[:], in_=acc[:])
             nc.sync.dma_start(out=out[r * P : (r + 1) * P, :], in_=res[:])
 
         blocks = {0: load_block(0), 1: load_block(1)}
         raws = [load_weights(c) for c in range(PASSES)]
-        fronts = {0: front(blocks[0])}
-        stages = {}
+        blocks[2] = load_block(2)
+        gated = {0: gates(blocks[0]), 1: gates(blocks[1])}
+        nats = {0: cell(gated[0])}
+        operands = {}
         for r in range(BLOCKS):
+            if r + 3 < BLOCKS:
+                blocks[r + 3] = load_block(r + 3)
             if r + 2 < BLOCKS:
-                blocks[r + 2] = load_block(r + 2)
+                gated[r + 2] = gates(blocks[r + 2])
             if r + 1 < BLOCKS:
-                fronts[r + 1] = front(blocks[r + 1])
-            stages[r] = stage_a(fronts[r])
-            if r < 2:
-                for c in range(3 * r, 3 * r + 3):
-                    quantise_weights(c, raws[c])
+                nats[r + 1] = cell(gated[r + 1])
+            da_i = cols_pool.tile([P, HALVES, P, PACK], BF16, align_bytes=64, bufs=2)
+            da_g = cols_pool.tile([P, HALVES, P, PACK], BF16, align_bytes=64, bufs=2)
+            da_o = cols_pool.tile([P, HALVES, P, PACK], BF16, align_bytes=64, bufs=2)
             if r >= 1:
-                multiply(r - 1, stage_b(stages[r - 1]))
-        multiply(BLOCKS - 1, stage_b(stages[BLOCKS - 1]))
+                acc = psum_o.tile([P, D], F32)
+            for h in range(HALVES):
+                products(nats[r], h, da_i, da_g, da_o)
+                if r == 0:
+                    for c in range(3 * h, 3 * h + 3):
+                        quantise_weights(c, raws[c])
+                if r >= 1:
+                    multiply(acc, operands[r - 1], range(3 * h, 3 * h + 3))
+            if r >= 1:
+                store(r - 1, acc)
+            operands[r] = [quantise("i", da_i), quantise("g", da_g), quantise("o", da_o)]
+        acc = psum_o.tile([P, D], F32)
+        multiply(acc, operands[BLOCKS - 1], range(PASSES))
+        store(BLOCKS - 1, acc)

@@ -19,29 +19,62 @@ B, D, H = 1024, 512, 1024
 BLOCKS = B // P
 HALVES = H // K_PASS
 GATE_ROW = (0, 2 * H, 3 * H)
-PASSES = len(GATE_ROW) * HALVES
+GATES = len(GATE_ROW)
+PASSES = GATES * HALVES
 
 FLOPS = 2 * B * 3 * H * D
 BYTES = 3 * B * H * 4 + B * H * 2 + 3 * H * D * 2 + B * D * 4
+
+
+def flat(tile_ap):
+    return tile_ap.rearrange("p h w t -> p (h w t)")
+
+
+def pieces_of_work():
+    pieces = []
+    for r in range(BLOCKS):
+        if r in (0, BLOCKS - 1):
+            pieces.extend([(r, h, 1) for h in range(HALVES)])
+        else:
+            pieces.append((r, 0, HALVES))
+    return pieces
 
 
 def tile_lstmbaseline_pa_v_kernel(tc, x, W_ih0, b_ih0, b_hh0, a_i, a_g, a_o, grad_out, out):
     nc = tc.nc
     with ExitStack() as ctx:
         const = ctx.enter_context(tc.tile_pool(name="const", bufs=1))
-        rows_pool = ctx.enter_context(tc.tile_pool(name="rows_pool", bufs=3))
-        cols_pool = ctx.enter_context(tc.tile_pool(name="cols_pool", bufs=3))
-        mxop = ctx.enter_context(tc.tile_pool(name="mxop", bufs=3))
+        loads = ctx.enter_context(tc.tile_pool(name="loads", bufs=3))
+        work = ctx.enter_context(tc.tile_pool(name="work", bufs=2))
+        mxop = ctx.enter_context(tc.tile_pool(name="mxop", bufs=4))
         wraw = ctx.enter_context(tc.tile_pool(name="wraw", bufs=PASSES))
-        psum_t = ctx.enter_context(tc.psum_pool(name="psum_t", bufs=1))
+        psum_a = ctx.enter_context(tc.psum_pool(name="psum_a", bufs=2))
+        psum_g = ctx.enter_context(tc.psum_pool(name="psum_g", bufs=1))
         psum_o = ctx.enter_context(tc.psum_pool(name="psum_o", bufs=1))
 
-        ident = const.tile([P, P], F32)
-        make_identity(nc, ident[:])
-        minus_half = const.tile([P, 1], F32)
-        nc.vector.memset(minus_half[:], -0.5)
+        ident_f32 = const.tile([P, P], F32)
+        make_identity(nc, ident_f32[:])
+        ident_bf16 = const.tile([P, P], BF16)
+        make_identity(nc, ident_bf16[:])
         w_codes = const.tile([P, PASSES, D], U32, align_bytes=64)
         w_scales = const.tile([P, PASSES, D], U8, align_bytes=64)
+
+        def stt(dst, in0, scalar, op0, in1):
+            nc.vector.scalar_tensor_tensor(out=dst, in0=in0, scalar=scalar, in1=in1, op0=op0, op1=ALU.mult)
+
+        def load_piece(piece):
+            r, h0, nh = piece
+            rows = slice(r * P, (r + 1) * P)
+            cols = slice(h0 * K_PASS, (h0 + nh) * K_PASS)
+            ai = loads.tile([P, nh * K_PASS], F32)
+            nc.sync.dma_start(out=ai[:], in_=a_i[rows, cols])
+            ag = loads.tile([P, nh * K_PASS], F32)
+            nc.sync.dma_start(out=ag[:], in_=a_g[rows, cols])
+            ao = loads.tile([P, nh * K_PASS], F32)
+            nc.sync.dma_start(out=ao[:], in_=a_o[rows, cols])
+            go = loads.tile([P, nh * K_PASS], BF16)
+            nc.sync.dma_start(out=go[:], in_=grad_out[rows, cols])
+            return ai, ag, ao, go
 
         def load_weights(c):
             row0 = GATE_ROW[c // HALVES] + (c % HALVES) * K_PASS
@@ -52,8 +85,8 @@ def tile_lstmbaseline_pa_v_kernel(tc, x, W_ih0, b_ih0, b_hh0, a_i, a_g, a_o, gra
             return raw
 
         def quantise_weights(c, raw):
-            grouped = cols_pool.tile([P, D, PACK], BF16, align_bytes=64, bufs=2)
-            nc.vector.tensor_copy(
+            grouped = work.tile([P, D, PACK], BF16, align_bytes=64)
+            nc.scalar.copy(
                 out=grouped[:].rearrange("p (c i) t -> p c t i", i=4),
                 in_=raw[:].rearrange("p t (c i) -> p c t i", i=4),
             )
@@ -63,131 +96,127 @@ def tile_lstmbaseline_pa_v_kernel(tc, x, W_ih0, b_ih0, b_hh0, a_i, a_g, a_o, gra
                 in_=grouped[:].rearrange("p n t -> p (n t)"),
             )
 
-        def load_block(r):
-            rows = slice(r * P, (r + 1) * P)
-            si = rows_pool.tile([P, H], F32, bufs=4)
-            nc.sync.dma_start(out=si[:], in_=a_i[rows, :])
-            tg = rows_pool.tile([P, H], F32)
-            nc.sync.dma_start(out=tg[:], in_=a_g[rows, :])
-            so = rows_pool.tile([P, H], F32, bufs=4)
-            nc.sync.dma_start(out=so[:], in_=a_o[rows, :])
-            go = rows_pool.tile([P, H], BF16, bufs=4)
-            nc.sync.dma_start(out=go[:], in_=grad_out[rows, :])
-            return si, tg, so, go
-
-        def gates(block):
-            si, tg, so, go = block
-            nc.scalar.activation(out=si[:], in_=si[:], func=FUNC.Sigmoid)
-            nc.scalar.activation(out=tg[:], in_=tg[:], func=FUNC.Tanh)
-            nc.scalar.activation(out=so[:], in_=so[:], func=FUNC.Sigmoid)
-            cc = rows_pool.tile([P, H], F32)
-            nc.gpsimd.tensor_tensor(out=cc[:], in0=si[:], in1=tg[:], op=ALU.mult)
-            gso = rows_pool.tile([P, H], F32)
-            nc.gpsimd.tensor_tensor(out=gso[:], in0=so[:], in1=go[:], op=ALU.mult)
-            return si, tg, so, go, cc, gso
-
-        def cell(gt):
-            si, tg, so, go, cc, gso = gt
-            ntc = rows_pool.tile([P, H], F32)
-            nc.scalar.activation(out=ntc[:], in_=cc[:], func=FUNC.Tanh, scale=-1.0)
-            tg2 = rows_pool.tile([P, H], F32)
-            nc.scalar.activation(out=tg2[:], in_=tg[:], func=FUNC.Square)
-            n1 = rows_pool.tile([P, H], F32)
-            nc.gpsimd.tensor_tensor(out=n1[:], in0=ntc[:], in1=go[:], op=ALU.mult)
-            return {"si": si, "so": so, "cc": cc, "gso": gso, "ntc": ntc, "tg2": tg2, "n1": n1}
-
-        def turned(nat, key, h):
-            bank = psum_t.tile([P, PACK, P], F32, name="bank_" + key, tag="bank_" + key)
+        def turned_tanh(src, dst, scale, h, bank):
             for t in range(PACK):
                 col0 = h * K_PASS + t * P
-                nc.tensor.transpose(bank[:, t, :], nat[key][:, col0 : col0 + P], ident[:])
-            return bank[:].rearrange("p t w -> p w t")
-
-        def products(nat, h, da_i, da_g, da_o):
-            so_t = turned(nat, "so", h)
-            sq_o = cols_pool.tile([P, P, PACK], F32)
-            nc.scalar.activation(out=sq_o[:], in_=so_t, func=FUNC.Square, bias=minus_half[:])
-            ntc_t = turned(nat, "ntc", h)
-            tc2 = cols_pool.tile([P, P, PACK], F32)
-            nc.scalar.activation(out=tc2[:], in_=ntc_t, func=FUNC.Square)
-            gso_t = turned(nat, "gso", h)
-            xx = cols_pool.tile([P, P, PACK], F32)
-            nc.vector.scalar_tensor_tensor(
-                out=xx[:], in0=tc2[:], scalar=-1.0, in1=gso_t, op0=ALU.add, op1=ALU.mult
-            )
-            n1_t = turned(nat, "n1", h)
-            nc.vector.scalar_tensor_tensor(
-                out=da_o[:, h], in0=sq_o[:], scalar=-0.25, in1=n1_t, op0=ALU.add, op1=ALU.mult
-            )
-            si_t = turned(nat, "si", h)
-            f1 = cols_pool.tile([P, P, PACK], F32)
-            nc.vector.scalar_tensor_tensor(
-                out=f1[:], in0=si_t, scalar=-1.0, in1=xx[:], op0=ALU.add, op1=ALU.mult
-            )
-            e1 = cols_pool.tile([P, P, PACK], F32)
-            nc.vector.tensor_tensor(out=e1[:], in0=si_t, in1=xx[:], op=ALU.mult)
-            cc_t = turned(nat, "cc", h)
-            nc.vector.tensor_tensor(out=da_i[:, h], in0=cc_t, in1=f1[:], op=ALU.mult)
-            tg2_t = turned(nat, "tg2", h)
-            nc.vector.scalar_tensor_tensor(
-                out=da_g[:, h], in0=tg2_t, scalar=-1.0, in1=e1[:], op0=ALU.add, op1=ALU.mult
+                nc.tensor.transpose(bank[:, t, :], src[:, col0 : col0 + P], ident_f32[:])
+            nc.scalar.activation(
+                out=dst[:, h], in_=bank[:].rearrange("p t w -> p w t"), func=FUNC.Tanh, scale=scale
             )
 
-        def quantise(key, da):
-            codes = mxop.tile([P, HALVES * P], U32, align_bytes=64, name="codes_" + key, tag="codes_" + key)
-            scales = mxop.tile([P, HALVES * P], U8, align_bytes=64, name="scales_" + key, tag="scales_" + key)
-            nc.vector.quantize_mx(
-                out=codes[:].bitcast(E5M2_X4), scales=scales[:], in_=da[:].rearrange("p h w t -> p (h w t)")
-            )
+        def front(piece, loaded):
+            nh = piece[2]
+            ai, ag, ao, go = loaded
+            ti = work.tile([P, nh, P, PACK], F32, bufs=3)
+            tg = work.tile([P, nh, P, PACK], F32)
+            to = work.tile([P, nh, P, PACK], F32)
+            g_t = psum_g.tile([P, nh, PACK, P], BF16)
+            for h in range(nh):
+                ai_t = psum_a.tile([P, PACK, P], F32)
+                turned_tanh(ai, ti, 0.5, h, ai_t)
+                ag_t = psum_a.tile([P, PACK, P], F32)
+                turned_tanh(ag, tg, 1.0, h, ag_t)
+                ao_t = psum_a.tile([P, PACK, P], F32)
+                turned_tanh(ao, to, 0.5, h, ao_t)
+                for t in range(PACK):
+                    col0 = h * K_PASS + t * P
+                    nc.tensor.transpose(g_t[:, h, t, :], go[:, col0 : col0 + P], ident_bf16[:])
+            return ti, tg, to, g_t
+
+        def stage_a(piece, fr):
+            nh = piece[2]
+            shape = [P, nh, P, PACK]
+            ti, tg, to, g_t = fr
+            u = work.tile(shape, F32)
+            stt(flat(u[:]), flat(ti[:]), 1.0, ALU.add, flat(tg[:]))
+            gs = work.tile(shape, F32)
+            for h in range(nh):
+                stt(gs[:, h], to[:, h], 1.0, ALU.add, g_t[:, h].rearrange("p t w -> p w t"))
+            t1 = work.tile(shape, F32)
+            stt(flat(t1[:]), flat(to[:]), -1.0, ALU.add, flat(gs[:]))
+            tch = work.tile(shape, F32)
+            nc.scalar.activation(out=flat(tch[:]), in_=flat(u[:]), func=FUNC.Tanh, scale=0.5)
+            tc2 = work.tile(shape, F32)
+            nc.scalar.activation(out=flat(tc2[:]), in_=flat(tch[:]), func=FUNC.Square)
+            tg2q = work.tile(shape, F32)
+            nc.scalar.activation(out=flat(tg2q[:]), in_=flat(tg[:]), func=FUNC.Square, scale=0.5)
+            return ti, u, gs, t1, tch, tc2, tg2q
+
+        def quantise(key, nh, da):
+            codes = mxop.tile([P, nh * P], U32, align_bytes=64, name="codes_" + key, tag="codes_" + key)
+            scales = mxop.tile([P, nh * P], U8, align_bytes=64, name="scales_" + key, tag="scales_" + key)
+            nc.vector.quantize_mx(out=codes[:].bitcast(E5M2_X4), scales=scales[:], in_=flat(da[:]))
             return codes, scales
 
-        def multiply(acc, operands, passes):
-            for c in passes:
-                codes, scales = operands[c // HALVES]
-                cols = slice((c % HALVES) * P, (c % HALVES + 1) * P)
+        def stage_b(piece, st):
+            nh = piece[2]
+            shape = [P, nh, P, PACK]
+            ti, u, gs, t1, tch, tc2, tg2q = st
+            xx = work.tile(shape, F32)
+            stt(flat(xx[:]), flat(tc2[:]), -1.0, ALU.add, flat(gs[:]))
+            da_o = work.tile(shape, BF16, align_bytes=64)
+            stt(flat(da_o[:]), flat(t1[:]), -0.25, ALU.mult, flat(tch[:]))
+            t2 = work.tile(shape, F32)
+            stt(flat(t2[:]), flat(xx[:]), 0.125, ALU.mult, flat(u[:]))
+            t3 = work.tile(shape, F32)
+            stt(flat(t3[:]), flat(tg2q[:]), -0.25, ALU.add, flat(xx[:]))
+            q_o = quantise("o", nh, da_o)
+            da_i = work.tile(shape, BF16, align_bytes=64)
+            stt(flat(da_i[:]), flat(ti[:]), -1.0, ALU.add, flat(t2[:]))
+            da_g = work.tile(shape, BF16, align_bytes=64)
+            stt(flat(da_g[:]), flat(ti[:]), 1.0, ALU.add, flat(t3[:]))
+            q_i = quantise("i", nh, da_i)
+            q_g = quantise("g", nh, da_g)
+            return {2: q_o, 0: q_i, 1: q_g}
+
+        open_acc = {}
+
+        def multiply(piece, operands):
+            r, h0, nh = piece
+            if h0 == 0:
+                acc = psum_o.tile([P, D], F32)
+                open_acc[r] = acc
+            acc = open_acc[r]
+            todo = [(gate, h) for gate in operands for h in range(nh)]
+            for n, (gate, h) in enumerate(todo):
+                codes, scales = operands[gate]
+                c = gate * HALVES + h0 + h
                 nc.tensor.matmul_mx(
                     out=acc[:],
-                    lhsT=codes[:, cols].bitcast(E5M2_X4),
-                    lhsT_scale=scales[:, cols],
+                    lhsT=codes[:, h * P : (h + 1) * P].bitcast(E5M2_X4),
+                    lhsT_scale=scales[:, h * P : (h + 1) * P],
                     rhs=w_codes[:, c, :].bitcast(E4M3_X4),
                     rhs_scale=w_scales[:, c, :],
-                    start=(c == 0),
-                    stop=(c == PASSES - 1),
+                    start=(h0 == 0 and n == 0),
+                    stop=(h0 + nh == HALVES and n == len(todo) - 1),
                 )
+            if h0 + nh == HALVES:
+                res = work.tile([P, D], F32)
+                nc.scalar.copy(out=res[:], in_=acc[:])
+                nc.sync.dma_start(out=out[r * P : (r + 1) * P, :], in_=res[:])
 
-        def store(r, acc):
-            res = cols_pool.tile([P, D], F32, bufs=2)
-            nc.scalar.copy(out=res[:], in_=acc[:])
-            nc.sync.dma_start(out=out[r * P : (r + 1) * P, :], in_=res[:])
-
-        blocks = {0: load_block(0), 1: load_block(1)}
+        pieces = pieces_of_work()
+        n_pieces = len(pieces)
+        loaded = {0: load_piece(pieces[0]), 1: load_piece(pieces[1]), 2: load_piece(pieces[2])}
         raws = [load_weights(c) for c in range(PASSES)]
-        blocks[2] = load_block(2)
-        gated = {0: gates(blocks[0]), 1: gates(blocks[1])}
-        nats = {0: cell(gated[0])}
+        fronts = {0: front(pieces[0], loaded[0])}
+        stages = {}
         operands = {}
-        for r in range(BLOCKS):
-            if r + 3 < BLOCKS:
-                blocks[r + 3] = load_block(r + 3)
-            if r + 2 < BLOCKS:
-                gated[r + 2] = gates(blocks[r + 2])
-            if r + 1 < BLOCKS:
-                nats[r + 1] = cell(gated[r + 1])
-            da_i = cols_pool.tile([P, HALVES, P, PACK], BF16, align_bytes=64, bufs=2)
-            da_g = cols_pool.tile([P, HALVES, P, PACK], BF16, align_bytes=64, bufs=2)
-            da_o = cols_pool.tile([P, HALVES, P, PACK], BF16, align_bytes=64, bufs=2)
-            if r >= 1:
-                acc = psum_o.tile([P, D], F32)
-            for h in range(HALVES):
-                products(nats[r], h, da_i, da_g, da_o)
-                if r == 0:
-                    for c in range(3 * h, 3 * h + 3):
-                        quantise_weights(c, raws[c])
-                if r >= 1:
-                    multiply(acc, operands[r - 1], range(3 * h, 3 * h + 3))
-            if r >= 1:
-                store(r - 1, acc)
-            operands[r] = [quantise("i", da_i), quantise("g", da_g), quantise("o", da_o)]
-        acc = psum_o.tile([P, D], F32)
-        multiply(acc, operands[BLOCKS - 1], range(PASSES))
-        store(BLOCKS - 1, acc)
+        multiplied = 0
+        for i in range(n_pieces + 1):
+            if i + 3 < n_pieces:
+                loaded[i + 3] = load_piece(pieces[i + 3])
+            if i + 1 < n_pieces:
+                fronts[i + 1] = front(pieces[i + 1], loaded[i + 1])
+            if i < n_pieces:
+                stages[i] = stage_a(pieces[i], fronts[i])
+            if i < GATES:
+                quantise_weights(2 * i, raws[2 * i])
+                quantise_weights(2 * i + 1, raws[2 * i + 1])
+            if i >= 1:
+                operands[i - 1] = stage_b(pieces[i - 1], stages[i - 1])
+            if i >= GATES:
+                ready = i if i == n_pieces else i - 1
+                for j in range(multiplied, ready):
+                    multiply(pieces[j], operands[j])
+                multiplied = ready

@@ -18,39 +18,54 @@ K_PASS = P * PACK
 B, D, H = 1024, 512, 1024
 BLOCKS = B // P
 HALVES = H // K_PASS
+PIECES = BLOCKS * HALVES
 GATE_ROW = (0, 2 * H, 3 * H)
 GATES = len(GATE_ROW)
 PASSES = GATES * HALVES
+SPLIT_BLOCKS = 2
+LOAD_BUFS = 4
+W_ORDER = (0, 2, 4, 1, 3, 5)
+W_ON_VECTOR = 2
+W_START = -1
+M_START = W_START + PASSES + 1
 
 FLOPS = 2 * B * 3 * H * D
 BYTES = 3 * B * H * 4 + B * H * 2 + 3 * H * D * 2 + B * D * 4
 
 
 def flat(tile_ap):
-    return tile_ap.rearrange("p h w t -> p (h w t)")
+    return tile_ap.rearrange("p w t -> p (w t)")
 
 
-def pieces_of_work():
-    pieces = []
+def turned(bank_ap):
+    return bank_ap.rearrange("p t w -> p w t")
+
+
+def load_units():
+    units = []
     for r in range(BLOCKS):
-        if r in (0, BLOCKS - 1):
-            pieces.extend([(r, h, 1) for h in range(HALVES)])
+        if r < SPLIT_BLOCKS:
+            units.extend([(r, h, 1) for h in range(HALVES)])
         else:
-            pieces.append((r, 0, HALVES))
-    return pieces
+            units.append((r, 0, HALVES))
+    return units
 
 
 def tile_lstmbaseline_pa_v_kernel(tc, x, W_ih0, b_ih0, b_hh0, a_i, a_g, a_o, grad_out, out):
     nc = tc.nc
     with ExitStack() as ctx:
         const = ctx.enter_context(tc.tile_pool(name="const", bufs=1))
-        loads = ctx.enter_context(tc.tile_pool(name="loads", bufs=3))
-        work = ctx.enter_context(tc.tile_pool(name="work", bufs=2))
-        mxop = ctx.enter_context(tc.tile_pool(name="mxop", bufs=4))
+        loads = ctx.enter_context(tc.tile_pool(name="loads", bufs=LOAD_BUFS))
+        work = ctx.enter_context(tc.tile_pool(name="work", bufs=3))
+        mxop = ctx.enter_context(tc.tile_pool(name="mxop", bufs=10))
         wraw = ctx.enter_context(tc.tile_pool(name="wraw", bufs=PASSES))
-        psum_a = ctx.enter_context(tc.psum_pool(name="psum_a", bufs=2))
-        psum_g = ctx.enter_context(tc.psum_pool(name="psum_g", bufs=1))
-        psum_o = ctx.enter_context(tc.psum_pool(name="psum_o", bufs=1))
+        ps_ag = ctx.enter_context(tc.psum_pool(name="ps_ag", bufs=1))
+        ps_g = ctx.enter_context(tc.psum_pool(name="ps_g", bufs=1))
+        ps_so = ctx.enter_context(tc.psum_pool(name="ps_so", bufs=1))
+        ps_s1 = ctx.enter_context(tc.psum_pool(name="ps_s1", bufs=1))
+        ps_s2 = ctx.enter_context(tc.psum_pool(name="ps_s2", bufs=2))
+        ps_acc = ctx.enter_context(tc.psum_pool(name="ps_acc", bufs=2))
+        ctx.enter_context(tc.manual_schedule())
 
         ident_f32 = const.tile([P, P], F32)
         make_identity(nc, ident_f32[:])
@@ -59,164 +74,238 @@ def tile_lstmbaseline_pa_v_kernel(tc, x, W_ih0, b_ih0, b_hh0, a_i, a_g, a_o, gra
         w_codes = const.tile([P, PASSES, D], U32, align_bytes=64)
         w_scales = const.tile([P, PASSES, D], U8, align_bytes=64)
 
-        def stt(dst, in0, scalar, op0, in1):
-            nc.vector.scalar_tensor_tensor(out=dst, in0=in0, scalar=scalar, in1=in1, op0=op0, op1=ALU.mult)
+        def wt(name, dtype, bufs):
+            return work.tile([P, P, PACK], dtype, name=name, tag=name, bufs=bufs, align_bytes=64)
 
-        def load_piece(piece):
-            r, h0, nh = piece
+        def stt(dst, in0, scalar, in1):
+            nc.vector.scalar_tensor_tensor(out=dst, in0=in0, scalar=scalar, in1=in1, op0=ALU.add, op1=ALU.mult)
+
+        units = load_units()
+        where = {}
+
+        def load_unit(u):
+            r, h0, nh = units[u]
             rows = slice(r * P, (r + 1) * P)
             cols = slice(h0 * K_PASS, (h0 + nh) * K_PASS)
-            ai = loads.tile([P, nh * K_PASS], F32)
-            nc.sync.dma_start(out=ai[:], in_=a_i[rows, cols])
-            ag = loads.tile([P, nh * K_PASS], F32)
-            nc.sync.dma_start(out=ag[:], in_=a_g[rows, cols])
-            ao = loads.tile([P, nh * K_PASS], F32)
-            nc.sync.dma_start(out=ao[:], in_=a_o[rows, cols])
-            go = loads.tile([P, nh * K_PASS], BF16)
-            nc.sync.dma_start(out=go[:], in_=grad_out[rows, cols])
-            return ai, ag, ao, go
+            tiles = {}
+            for key, src, dtype in (("ao", a_o, F32), ("ai", a_i, F32), ("go", grad_out, BF16), ("ag", a_g, F32)):
+                t = loads.tile([P, nh * K_PASS], dtype, name="ld_" + key, tag="ld_" + key)
+                nc.sync.dma_start(out=t[:], in_=src[rows, cols])
+                tiles[key] = t
+            for h in range(nh):
+                where[r * HALVES + h0 + h] = (tiles, h * K_PASS)
+
+        last_piece_of_unit = {(r * HALVES + h0 + nh - 1): u for u, (r, h0, nh) in enumerate(units)}
+
+        raws = {}
 
         def load_weights(c):
             row0 = GATE_ROW[c // HALVES] + (c % HALVES) * K_PASS
-            raw = wraw.tile([P, PACK, D], BF16)
+            raw = wraw.tile([P, PACK, D], BF16, name="wraw", tag="wraw")
             nc.sync.dma_start(
                 out=raw[:], in_=W_ih0[row0 : row0 + K_PASS, :].rearrange("(t p) n -> p t n", p=P)
             )
-            return raw
+            raws[c] = raw
 
-        def quantise_weights(c, raw):
-            grouped = work.tile([P, D, PACK], BF16, align_bytes=64)
-            nc.scalar.copy(
-                out=grouped[:].rearrange("p (c i) t -> p c t i", i=4),
-                in_=raw[:].rearrange("p t (c i) -> p c t i", i=4),
-            )
+        grouped_of = {}
+
+        def interleave_weights(c, on_vector):
+            grouped = work.tile([P, D, PACK], BF16, name="grouped", tag="grouped", bufs=3, align_bytes=64)
+            dst = grouped[:].rearrange("p (c i) t -> p c t i", i=4)
+            src = raws[c][:].rearrange("p t (c i) -> p c t i", i=4)
+            if on_vector:
+                nc.vector.tensor_copy(out=dst, in_=src)
+            else:
+                nc.scalar.copy(out=dst, in_=src)
+            grouped_of[c] = grouped
+
+        def quantise_weights(c):
             nc.vector.quantize_mx(
                 out=w_codes[:, c, :].bitcast(E4M3_X4),
                 scales=w_scales[:, c, :],
-                in_=grouped[:].rearrange("p n t -> p (n t)"),
+                in_=grouped_of[c][:].rearrange("p n t -> p (n t)"),
             )
 
-        def turned_tanh(src, dst, scale, h, bank):
+        S = {}
+
+        def transpose4(bank, src, col0, ident):
             for t in range(PACK):
-                col0 = h * K_PASS + t * P
-                nc.tensor.transpose(bank[:, t, :], src[:, col0 : col0 + P], ident_f32[:])
-            nc.scalar.activation(
-                out=dst[:, h], in_=bank[:].rearrange("p t w -> p w t"), func=FUNC.Tanh, scale=scale
-            )
+                nc.tensor.transpose(bank[:, t, :], src[:, col0 + t * P : col0 + (t + 1) * P], ident[:])
 
-        def front(piece, loaded):
-            nh = piece[2]
-            ai, ag, ao, go = loaded
-            ti = work.tile([P, nh, P, PACK], F32, bufs=3)
-            tg = work.tile([P, nh, P, PACK], F32)
-            to = work.tile([P, nh, P, PACK], F32)
-            g_t = psum_g.tile([P, nh, PACK, P], BF16)
-            for h in range(nh):
-                ai_t = psum_a.tile([P, PACK, P], F32)
-                turned_tanh(ai, ti, 0.5, h, ai_t)
-                ag_t = psum_a.tile([P, PACK, P], F32)
-                turned_tanh(ag, tg, 1.0, h, ag_t)
-                ao_t = psum_a.tile([P, PACK, P], F32)
-                turned_tanh(ao, to, 0.5, h, ao_t)
-                for t in range(PACK):
-                    col0 = h * K_PASS + t * P
-                    nc.tensor.transpose(g_t[:, h, t, :], go[:, col0 : col0 + P], ident_bf16[:])
-            return ti, tg, to, g_t
+        def t_raw(j):
+            tiles, c0 = where[j]
+            g_ps = ps_g.tile([P, PACK, P], BF16, name="g_ps")
+            transpose4(g_ps, tiles["go"], c0, ident_bf16)
+            ag_t = ps_ag.tile([P, PACK, P], F32, name="ag_t")
+            transpose4(ag_t, tiles["ag"], c0, ident_f32)
+            S["g_ps", j] = g_ps
+            S["ag_t", j] = ag_t
 
-        def stage_a(piece, fr):
-            nh = piece[2]
-            shape = [P, nh, P, PACK]
-            ti, tg, to, g_t = fr
-            u = work.tile(shape, F32)
-            stt(flat(u[:]), flat(ti[:]), 1.0, ALU.add, flat(tg[:]))
-            gs = work.tile(shape, F32)
-            for h in range(nh):
-                stt(gs[:, h], to[:, h], 1.0, ALU.add, g_t[:, h].rearrange("p t w -> p w t"))
-            t1 = work.tile(shape, F32)
-            stt(flat(t1[:]), flat(to[:]), -1.0, ALU.add, flat(gs[:]))
-            tch = work.tile(shape, F32)
-            nc.scalar.activation(out=flat(tch[:]), in_=flat(u[:]), func=FUNC.Tanh, scale=0.5)
-            tc2 = work.tile(shape, F32)
-            nc.scalar.activation(out=flat(tc2[:]), in_=flat(tch[:]), func=FUNC.Square)
-            tg2q = work.tile(shape, F32)
-            nc.scalar.activation(out=flat(tg2q[:]), in_=flat(tg[:]), func=FUNC.Square, scale=0.5)
-            return ti, u, gs, t1, tch, tc2, tg2q
+        def act_a(j):
+            tiles, c0 = where[j]
+            so_n = work.tile([P, K_PASS], F32, name="so_n", tag="so_n", bufs=2)
+            nc.scalar.activation(out=so_n[:], in_=tiles["ao"][:, c0 : c0 + K_PASS], func=FUNC.Sigmoid)
+            si_n = work.tile([P, K_PASS], F32, name="si_n", tag="si_n", bufs=4)
+            nc.scalar.activation(out=si_n[:], in_=tiles["ai"][:, c0 : c0 + K_PASS], func=FUNC.Sigmoid)
+            S["so_n", j] = so_n
+            S["si_n", j] = si_n
 
-        def quantise(key, nh, da):
-            codes = mxop.tile([P, nh * P], U32, align_bytes=64, name="codes_" + key, tag="codes_" + key)
-            scales = mxop.tile([P, nh * P], U8, align_bytes=64, name="scales_" + key, tag="scales_" + key)
-            nc.vector.quantize_mx(out=codes[:].bitcast(E5M2_X4), scales=scales[:], in_=flat(da[:]))
-            return codes, scales
+        def act_b(j):
+            g_t = wt("g_t", BF16, 3)
+            nc.scalar.copy(out=g_t[:], in_=turned(S["g_ps", j][:]))
+            tg = wt("tg", F32, 4)
+            nc.scalar.activation(out=tg[:], in_=turned(S["ag_t", j][:]), func=FUNC.Tanh)
+            S["g_t", j] = g_t
+            S["tg", j] = tg
 
-        def stage_b(piece, st):
-            nh = piece[2]
-            shape = [P, nh, P, PACK]
-            ti, u, gs, t1, tch, tc2, tg2q = st
-            xx = work.tile(shape, F32)
-            stt(flat(xx[:]), flat(tc2[:]), -1.0, ALU.add, flat(gs[:]))
-            da_o = work.tile(shape, BF16, align_bytes=64)
-            stt(flat(da_o[:]), flat(t1[:]), -0.25, ALU.mult, flat(tch[:]))
-            t2 = work.tile(shape, F32)
-            stt(flat(t2[:]), flat(xx[:]), 0.125, ALU.mult, flat(u[:]))
-            t3 = work.tile(shape, F32)
-            stt(flat(t3[:]), flat(tg2q[:]), -0.25, ALU.add, flat(xx[:]))
-            q_o = quantise("o", nh, da_o)
-            da_i = work.tile(shape, BF16, align_bytes=64)
-            stt(flat(da_i[:]), flat(ti[:]), -1.0, ALU.add, flat(t2[:]))
-            da_g = work.tile(shape, BF16, align_bytes=64)
-            stt(flat(da_g[:]), flat(ti[:]), 1.0, ALU.add, flat(t3[:]))
-            q_i = quantise("i", nh, da_i)
-            q_g = quantise("g", nh, da_g)
-            return {2: q_o, 0: q_i, 1: q_g}
+        def t_act(j):
+            so_t = ps_so.tile([P, PACK, P], F32, name="so_t")
+            transpose4(so_t, S["so_n", j], 0, ident_f32)
+            s1_t = ps_s1.tile([P, PACK, P], F32, name="s1_t")
+            transpose4(s1_t, S["si_n", j], 0, ident_f32)
+            S["so_t", j] = so_t
+            S["s1_t", j] = s1_t
+
+        def t_again(j):
+            s2_t = ps_s2.tile([P, PACK, P], F32, name="s2_t")
+            transpose4(s2_t, S["si_n", j], 0, ident_f32)
+            S["s2_t", j] = s2_t
+
+        def dve_c(j):
+            gs = wt("gs", F32, 4)
+            nc.vector.tensor_tensor(out=gs[:], in0=turned(S["so_t", j][:]), in1=S["g_t", j][:], op=ALU.mult)
+            c = wt("c", F32, 4)
+            nc.vector.tensor_tensor(out=c[:], in0=turned(S["s1_t", j][:]), in1=S["tg", j][:], op=ALU.mult)
+            t1 = wt("t1", F32, 4)
+            stt(t1[:], turned(S["so_t", j][:]), -1.0, gs[:])
+            S["gs", j] = gs
+            S["c", j] = c
+            S["t1", j] = t1
+
+        def act_d(j):
+            tchn = wt("tchn", F32, 3)
+            nc.scalar.activation(out=flat(tchn[:]), in_=flat(S["c", j][:]), func=FUNC.Tanh, scale=-1.0)
+            tg2 = wt("tg2", F32, 4)
+            nc.scalar.activation(out=flat(tg2[:]), in_=flat(S["tg", j][:]), func=FUNC.Square)
+            tc2 = wt("tc2", F32, 3)
+            nc.scalar.activation(out=flat(tc2[:]), in_=flat(tchn[:]), func=FUNC.Square)
+            S["tchn", j] = tchn
+            S["tg2", j] = tg2
+            S["tc2", j] = tc2
+
+        def dve_xx(j):
+            xx = wt("xx", F32, 3)
+            stt(flat(xx[:]), flat(S["tc2", j][:]), -1.0, flat(S["gs", j][:]))
+            S["xx", j] = xx
+
+        def dve_t3(j):
+            t3 = wt("t3", F32, 2)
+            stt(flat(t3[:]), flat(S["tg2", j][:]), -1.0, flat(S["xx", j][:]))
+            S["t3", j] = t3
+
+        def pool_f(j):
+            t2 = wt("t2", F32, 2)
+            nc.gpsimd.tensor_tensor(out=flat(t2[:]), in0=flat(S["xx", j][:]), in1=flat(S["c", j][:]), op=ALU.mult)
+            da_o = wt("da_o", BF16, 3)
+            nc.gpsimd.tensor_tensor(out=flat(da_o[:]), in0=flat(S["t1", j][:]), in1=flat(S["tchn", j][:]), op=ALU.mult)
+            S["t2", j] = t2
+            S["da_o", j] = da_o
+
+        def dve_da_g(j):
+            da_g = wt("da_g", BF16, 3)
+            nc.vector.tensor_tensor(out=da_g[:], in0=turned(S["s2_t", j][:]), in1=S["t3", j][:], op=ALU.mult)
+            S["da_g", j] = da_g
+
+        def dve_da_i(j):
+            da_i = wt("da_i", BF16, 3)
+            stt(da_i[:], turned(S["s2_t", j][:]), -1.0, S["t2", j][:])
+            S["da_i", j] = da_i
+
+        def quantise(key, j):
+            codes = mxop.tile([P, P], U32, align_bytes=64, name="codes_" + key, tag="codes_" + key)
+            scales = mxop.tile([P, P], U8, align_bytes=64, name="scales_" + key, tag="scales_" + key)
+            nc.vector.quantize_mx(out=codes[:].bitcast(E5M2_X4), scales=scales[:], in_=flat(S["da_" + key, j][:]))
+            S["q_" + key, j] = (codes, scales)
 
         open_acc = {}
 
-        def multiply(piece, operands):
-            r, h0, nh = piece
-            if h0 == 0:
-                acc = psum_o.tile([P, D], F32)
+        def multiply(j):
+            r, h = divmod(j, HALVES)
+            if h == 0:
+                acc = ps_acc.tile([P, D], F32, name="acc")
                 open_acc[r] = acc
             acc = open_acc[r]
-            todo = [(gate, h) for gate in operands for h in range(nh)]
-            for n, (gate, h) in enumerate(todo):
-                codes, scales = operands[gate]
-                c = gate * HALVES + h0 + h
+            for n, (key, gate) in enumerate((("o", 2), ("i", 0), ("g", 1))):
+                codes, scales = S["q_" + key, j]
+                c = gate * HALVES + h
                 nc.tensor.matmul_mx(
                     out=acc[:],
-                    lhsT=codes[:, h * P : (h + 1) * P].bitcast(E5M2_X4),
-                    lhsT_scale=scales[:, h * P : (h + 1) * P],
+                    lhsT=codes[:].bitcast(E5M2_X4),
+                    lhsT_scale=scales[:],
                     rhs=w_codes[:, c, :].bitcast(E4M3_X4),
                     rhs_scale=w_scales[:, c, :],
-                    start=(h0 == 0 and n == 0),
-                    stop=(h0 + nh == HALVES and n == len(todo) - 1),
+                    start=(h == 0 and n == 0),
+                    stop=(h == HALVES - 1 and n == GATES - 1),
                 )
-            if h0 + nh == HALVES:
-                res = work.tile([P, D], F32)
+            if h == HALVES - 1:
+                res = work.tile([P, D], F32, name="res", tag="res", bufs=2)
                 nc.scalar.copy(out=res[:], in_=acc[:])
                 nc.sync.dma_start(out=out[r * P : (r + 1) * P, :], in_=res[:])
 
-        pieces = pieces_of_work()
-        n_pieces = len(pieces)
-        loaded = {0: load_piece(pieces[0]), 1: load_piece(pieces[1]), 2: load_piece(pieces[2])}
-        raws = [load_weights(c) for c in range(PASSES)]
-        fronts = {0: front(pieces[0], loaded[0])}
-        stages = {}
-        operands = {}
-        multiplied = 0
-        for i in range(n_pieces + 1):
-            if i + 3 < n_pieces:
-                loaded[i + 3] = load_piece(pieces[i + 3])
-            if i + 1 < n_pieces:
-                fronts[i + 1] = front(pieces[i + 1], loaded[i + 1])
-            if i < n_pieces:
-                stages[i] = stage_a(pieces[i], fronts[i])
-            if i < GATES:
-                quantise_weights(2 * i, raws[2 * i])
-                quantise_weights(2 * i + 1, raws[2 * i + 1])
-            if i >= 1:
-                operands[i - 1] = stage_b(pieces[i - 1], stages[i - 1])
-            if i >= GATES:
-                ready = i if i == n_pieces else i - 1
-                for j in range(multiplied, ready):
-                    multiply(pieces[j], operands[j])
-                multiplied = ready
+        def ok(j):
+            return 0 <= j < PIECES
+
+        load_unit(0)
+        load_unit(1)
+        load_weights(W_ORDER[0])
+        load_unit(2)
+        load_weights(W_ORDER[1])
+        load_unit(3)
+        for c in W_ORDER[2:]:
+            load_weights(c)
+
+        m_next = 0
+        for k in range(-3, PIECES + 3 + 2):
+            if ok(k + 3):
+                t_raw(k + 3)
+            wi = k - W_START
+            if 0 <= wi < W_ON_VECTOR:
+                interleave_weights(W_ORDER[wi], True)
+            if 0 <= wi - 1 < PASSES:
+                quantise_weights(W_ORDER[wi - 1])
+            if ok(k - 1):
+                quantise("o", k - 1)
+                quantise("i", k - 1)
+            if ok(k - 2):
+                quantise("g", k - 2)
+            if ok(k - 1):
+                dve_t3(k - 1)
+            if ok(k):
+                dve_xx(k)
+                pool_f(k)
+            if ok(k + 1):
+                act_d(k + 1)
+            if ok(k + 3):
+                act_a(k + 3)
+                act_b(k + 3)
+            if W_ON_VECTOR <= wi < PASSES:
+                interleave_weights(W_ORDER[wi], False)
+            if k >= M_START:
+                done = 0
+                while m_next < PIECES and m_next <= k - 2 and done < 3:
+                    multiply(m_next)
+                    m_next += 1
+                    done += 1
+            if ok(k + 2):
+                dve_c(k + 2)
+            if ok(k - 1):
+                dve_da_g(k - 1)
+            if ok(k):
+                dve_da_i(k)
+            if ok(k + 3):
+                t_act(k + 3)
+            if ok(k + 1):
+                t_again(k + 1)
+            u = last_piece_of_unit.get(k + 3)
+            if u is not None and u + LOAD_BUFS < len(units):
+                load_unit(u + LOAD_BUFS)

@@ -25,9 +25,10 @@ PASSES = GATES * HALVES
 SPLIT_BLOCKS = 2
 LOAD_BUFS = 4
 W_ORDER = (0, 2, 4, 1, 3, 5)
-W_ON_VECTOR = 2
-W_START = -1
-M_START = W_START + PASSES + 1
+W_PARTS = 2
+W_START = 0
+M_START = W_START + 10
+LAST_ON_VECTOR = 2
 
 FLOPS = 2 * B * 3 * H * D
 BYTES = 3 * B * H * 4 + B * H * 2 + 3 * H * D * 2 + B * D * 4
@@ -57,13 +58,12 @@ def tile_lstmbaseline_pa_v_kernel(tc, x, W_ih0, b_ih0, b_hh0, a_i, a_g, a_o, gra
         const = ctx.enter_context(tc.tile_pool(name="const", bufs=1))
         loads = ctx.enter_context(tc.tile_pool(name="loads", bufs=LOAD_BUFS))
         work = ctx.enter_context(tc.tile_pool(name="work", bufs=3))
-        mxop = ctx.enter_context(tc.tile_pool(name="mxop", bufs=10))
+        mxop = ctx.enter_context(tc.tile_pool(name="mxop", bufs=12))
         wraw = ctx.enter_context(tc.tile_pool(name="wraw", bufs=PASSES))
         ps_ag = ctx.enter_context(tc.psum_pool(name="ps_ag", bufs=1))
         ps_g = ctx.enter_context(tc.psum_pool(name="ps_g", bufs=1))
-        ps_so = ctx.enter_context(tc.psum_pool(name="ps_so", bufs=1))
-        ps_s1 = ctx.enter_context(tc.psum_pool(name="ps_s1", bufs=1))
-        ps_s2 = ctx.enter_context(tc.psum_pool(name="ps_s2", bufs=2))
+        ps_so = ctx.enter_context(tc.psum_pool(name="ps_so", bufs=2))
+        ps_si = ctx.enter_context(tc.psum_pool(name="ps_si", bufs=2))
         ps_acc = ctx.enter_context(tc.psum_pool(name="ps_acc", bufs=2))
         ctx.enter_context(tc.manual_schedule())
 
@@ -98,33 +98,53 @@ def tile_lstmbaseline_pa_v_kernel(tc, x, W_ih0, b_ih0, b_hh0, a_i, a_g, a_o, gra
         last_piece_of_unit = {(r * HALVES + h0 + nh - 1): u for u, (r, h0, nh) in enumerate(units)}
 
         raws = {}
+        w_to_load = list(W_ORDER)
 
-        def load_weights(c):
-            row0 = GATE_ROW[c // HALVES] + (c % HALVES) * K_PASS
-            raw = wraw.tile([P, PACK, D], BF16, name="wraw", tag="wraw")
-            nc.sync.dma_start(
-                out=raw[:], in_=W_ih0[row0 : row0 + K_PASS, :].rearrange("(t p) n -> p t n", p=P)
-            )
-            raws[c] = raw
+        def load_weights(count):
+            for c in list(w_to_load[:count]):
+                row0 = GATE_ROW[c // HALVES] + (c % HALVES) * K_PASS
+                raw = wraw.tile([P, PACK, D], BF16, name="wraw", tag="wraw")
+                nc.sync.dma_start(
+                    out=raw[:], in_=W_ih0[row0 : row0 + K_PASS, :].rearrange("(t p) n -> p t n", p=P)
+                )
+                raws[c] = raw
+                w_to_load.remove(c)
 
         grouped_of = {}
+        W_COLS = D // W_PARTS
 
-        def interleave_weights(c, on_vector):
-            grouped = work.tile([P, D, PACK], BF16, name="grouped", tag="grouped", bufs=3, align_bytes=64)
+        def interleave_weights(i, on_vector):
+            c, part = W_ORDER[i // W_PARTS], i % W_PARTS
+            grouped = work.tile([P, W_COLS, PACK], BF16, name="grouped", tag="grouped", bufs=4, align_bytes=64)
             dst = grouped[:].rearrange("p (c i) t -> p c t i", i=4)
-            src = raws[c][:].rearrange("p t (c i) -> p c t i", i=4)
+            src = raws[c][:, :, part * W_COLS : (part + 1) * W_COLS].rearrange("p t (c i) -> p c t i", i=4)
             if on_vector:
                 nc.vector.tensor_copy(out=dst, in_=src)
             else:
                 nc.scalar.copy(out=dst, in_=src)
-            grouped_of[c] = grouped
+            grouped_of[i] = grouped
 
-        def quantise_weights(c):
+        def quantise_weights(i):
+            c, part = W_ORDER[i // W_PARTS], i % W_PARTS
+            cols = slice(part * W_COLS, (part + 1) * W_COLS)
             nc.vector.quantize_mx(
-                out=w_codes[:, c, :].bitcast(E4M3_X4),
-                scales=w_scales[:, c, :],
-                in_=grouped_of[c][:].rearrange("p n t -> p (n t)"),
+                out=w_codes[:, c, cols].bitcast(E4M3_X4),
+                scales=w_scales[:, c, cols],
+                in_=grouped_of[i][:].rearrange("p n t -> p (n t)"),
             )
+
+        w_scalar = {}
+        w_vector = {}
+        w_quant = {}
+        for i in range(PASSES * W_PARTS):
+            if i % 3 == 2:
+                cyc = W_START + (i // 3) * 2 + 1
+                w_vector[cyc] = i
+                w_quant.setdefault(cyc + 1, []).append(i)
+            else:
+                cyc = W_START + (i // 3) * 2 + i % 3
+                w_scalar[cyc] = i
+                w_quant.setdefault(cyc + 2, []).append(i)
 
         S = {}
 
@@ -132,94 +152,81 @@ def tile_lstmbaseline_pa_v_kernel(tc, x, W_ih0, b_ih0, b_hh0, a_i, a_g, a_o, gra
             for t in range(PACK):
                 nc.tensor.transpose(bank[:, t, :], src[:, col0 + t * P : col0 + (t + 1) * P], ident[:])
 
-        def t_raw(j):
+        def pe_turn(j):
             tiles, c0 = where[j]
             g_ps = ps_g.tile([P, PACK, P], BF16, name="g_ps")
             transpose4(g_ps, tiles["go"], c0, ident_bf16)
             ag_t = ps_ag.tile([P, PACK, P], F32, name="ag_t")
             transpose4(ag_t, tiles["ag"], c0, ident_f32)
-            S["g_ps", j] = g_ps
-            S["ag_t", j] = ag_t
-
-        def act_a(j):
-            tiles, c0 = where[j]
-            so_n = work.tile([P, K_PASS], F32, name="so_n", tag="so_n", bufs=2)
-            nc.scalar.activation(out=so_n[:], in_=tiles["ao"][:, c0 : c0 + K_PASS], func=FUNC.Sigmoid)
-            si_n = work.tile([P, K_PASS], F32, name="si_n", tag="si_n", bufs=4)
-            nc.scalar.activation(out=si_n[:], in_=tiles["ai"][:, c0 : c0 + K_PASS], func=FUNC.Sigmoid)
-            S["so_n", j] = so_n
-            S["si_n", j] = si_n
-
-        def act_b(j):
-            g_t = wt("g_t", BF16, 3)
-            nc.scalar.copy(out=g_t[:], in_=turned(S["g_ps", j][:]))
-            tg = wt("tg", F32, 4)
-            nc.scalar.activation(out=tg[:], in_=turned(S["ag_t", j][:]), func=FUNC.Tanh)
-            S["g_t", j] = g_t
-            S["tg", j] = tg
-
-        def t_act(j):
             so_t = ps_so.tile([P, PACK, P], F32, name="so_t")
             transpose4(so_t, S["so_n", j], 0, ident_f32)
-            s1_t = ps_s1.tile([P, PACK, P], F32, name="s1_t")
-            transpose4(s1_t, S["si_n", j], 0, ident_f32)
+            si_t = ps_si.tile([P, PACK, P], F32, name="si_t")
+            transpose4(si_t, S["si_n", j], 0, ident_f32)
+            S["g_ps", j] = g_ps
+            S["ag_t", j] = ag_t
             S["so_t", j] = so_t
-            S["s1_t", j] = s1_t
+            S["si_t", j] = si_t
 
-        def t_again(j):
-            s2_t = ps_s2.tile([P, PACK, P], F32, name="s2_t")
-            transpose4(s2_t, S["si_n", j], 0, ident_f32)
-            S["s2_t", j] = s2_t
+        def scalar_cycle(jd, jb, ja):
+            if ok(jd):
+                tchn = wt("tchn", F32, 3)
+                nc.scalar.activation(out=flat(tchn[:]), in_=flat(S["c", jd][:]), func=FUNC.Tanh, scale=-1.0)
+                S["tchn", jd] = tchn
+            if ok(jb):
+                g_t = wt("g_t", BF16, 3)
+                nc.scalar.copy(out=g_t[:], in_=turned(S["g_ps", jb][:]))
+                S["g_t", jb] = g_t
+            if ok(jd):
+                tc2 = wt("tc2", F32, 3)
+                nc.scalar.activation(out=flat(tc2[:]), in_=flat(S["tchn", jd][:]), func=FUNC.Square)
+                S["tc2", jd] = tc2
+            if ok(jb):
+                tg = wt("tg", F32, 3)
+                nc.scalar.activation(out=tg[:], in_=turned(S["ag_t", jb][:]), func=FUNC.Tanh)
+                S["tg", jb] = tg
+            if ok(ja):
+                tiles, c0 = where[ja]
+                so_n = work.tile([P, K_PASS], F32, name="so_n", tag="so_n", bufs=3)
+                nc.scalar.activation(out=so_n[:], in_=tiles["ao"][:, c0 : c0 + K_PASS], func=FUNC.Sigmoid)
+                S["so_n", ja] = so_n
+            if ok(jb):
+                tg2 = wt("tg2", F32, 3)
+                nc.scalar.activation(out=flat(tg2[:]), in_=flat(S["tg", jb][:]), func=FUNC.Square)
+                S["tg2", jb] = tg2
+            if ok(ja):
+                tiles, c0 = where[ja]
+                si_n = work.tile([P, K_PASS], F32, name="si_n", tag="si_n", bufs=3)
+                nc.scalar.activation(out=si_n[:], in_=tiles["ai"][:, c0 : c0 + K_PASS], func=FUNC.Sigmoid)
+                S["si_n", ja] = si_n
 
-        def dve_c(j):
+        def vector_early(j):
+            so_t = turned(S["so_t", j][:])
+            si_t = turned(S["si_t", j][:])
             gs = wt("gs", F32, 4)
-            nc.vector.tensor_tensor(out=gs[:], in0=turned(S["so_t", j][:]), in1=S["g_t", j][:], op=ALU.mult)
-            c = wt("c", F32, 4)
-            nc.vector.tensor_tensor(out=c[:], in0=turned(S["s1_t", j][:]), in1=S["tg", j][:], op=ALU.mult)
+            nc.vector.tensor_tensor(out=gs[:], in0=so_t, in1=S["g_t", j][:], op=ALU.mult)
+            c = wt("c", F32, 3)
+            nc.vector.tensor_tensor(out=c[:], in0=si_t, in1=S["tg", j][:], op=ALU.mult)
             t1 = wt("t1", F32, 4)
-            stt(t1[:], turned(S["so_t", j][:]), -1.0, gs[:])
+            stt(t1[:], so_t, -1.0, gs[:])
+            v2 = wt("v2", F32, 5)
+            stt(v2[:], S["tg2", j][:], -1.0, si_t)
+            v1 = wt("v1", F32, 4)
+            stt(v1[:], si_t, -1.0, c[:])
             S["gs", j] = gs
             S["c", j] = c
             S["t1", j] = t1
+            S["v1", j] = v1
+            S["v2", j] = v2
 
-        def act_d(j):
-            tchn = wt("tchn", F32, 3)
-            nc.scalar.activation(out=flat(tchn[:]), in_=flat(S["c", j][:]), func=FUNC.Tanh, scale=-1.0)
-            tg2 = wt("tg2", F32, 4)
-            nc.scalar.activation(out=flat(tg2[:]), in_=flat(S["tg", j][:]), func=FUNC.Square)
-            tc2 = wt("tc2", F32, 3)
-            nc.scalar.activation(out=flat(tc2[:]), in_=flat(tchn[:]), func=FUNC.Square)
-            S["tchn", j] = tchn
-            S["tg2", j] = tg2
-            S["tc2", j] = tc2
-
-        def dve_xx(j):
+        def vector_xx(j):
             xx = wt("xx", F32, 3)
             stt(flat(xx[:]), flat(S["tc2", j][:]), -1.0, flat(S["gs", j][:]))
             S["xx", j] = xx
 
-        def dve_t3(j):
-            t3 = wt("t3", F32, 2)
-            stt(flat(t3[:]), flat(S["tg2", j][:]), -1.0, flat(S["xx", j][:]))
-            S["t3", j] = t3
-
-        def pool_f(j):
-            t2 = wt("t2", F32, 2)
-            nc.gpsimd.tensor_tensor(out=flat(t2[:]), in0=flat(S["xx", j][:]), in1=flat(S["c", j][:]), op=ALU.mult)
-            da_o = wt("da_o", BF16, 3)
-            nc.gpsimd.tensor_tensor(out=flat(da_o[:]), in0=flat(S["t1", j][:]), in1=flat(S["tchn", j][:]), op=ALU.mult)
-            S["t2", j] = t2
-            S["da_o", j] = da_o
-
-        def dve_da_g(j):
-            da_g = wt("da_g", BF16, 3)
-            nc.vector.tensor_tensor(out=da_g[:], in0=turned(S["s2_t", j][:]), in1=S["t3", j][:], op=ALU.mult)
-            S["da_g", j] = da_g
-
-        def dve_da_i(j):
-            da_i = wt("da_i", BF16, 3)
-            stt(da_i[:], turned(S["s2_t", j][:]), -1.0, S["t2", j][:])
-            S["da_i", j] = da_i
+        def product(engine, key, j, a, b):
+            da = wt("da_" + key, BF16, 3)
+            engine.tensor_tensor(out=flat(da[:]), in0=flat(S[a, j][:]), in1=flat(S[b, j][:]), op=ALU.mult)
+            S["da_" + key, j] = da
 
         def quantise(key, j):
             codes = mxop.tile([P, P], U32, align_bytes=64, name="codes_" + key, tag="codes_" + key)
@@ -255,57 +262,44 @@ def tile_lstmbaseline_pa_v_kernel(tc, x, W_ih0, b_ih0, b_hh0, a_i, a_g, a_o, gra
         def ok(j):
             return 0 <= j < PIECES
 
-        load_unit(0)
-        load_unit(1)
-        load_weights(W_ORDER[0])
-        load_unit(2)
-        load_weights(W_ORDER[1])
-        load_unit(3)
-        for c in W_ORDER[2:]:
-            load_weights(c)
+        for u in range(LOAD_BUFS):
+            load_unit(u)
+        load_weights(2)
 
         m_next = 0
-        for k in range(-3, PIECES + 3 + 2):
+        for k in range(-4, PIECES + 6):
             if ok(k + 3):
-                t_raw(k + 3)
-            wi = k - W_START
-            if 0 <= wi < W_ON_VECTOR:
-                interleave_weights(W_ORDER[wi], True)
-            if 0 <= wi - 1 < PASSES:
-                quantise_weights(W_ORDER[wi - 1])
+                pe_turn(k + 3)
             if ok(k - 1):
+                product(nc.vector, "g", k - 1, "xx", "v2")
                 quantise("o", k - 1)
                 quantise("i", k - 1)
-            if ok(k - 2):
-                quantise("g", k - 2)
+            if k in w_vector:
+                interleave_weights(w_vector[k], True)
+            for i in w_quant.get(k, []):
+                quantise_weights(i)
             if ok(k - 1):
-                dve_t3(k - 1)
+                quantise("g", k - 1)
             if ok(k):
-                dve_xx(k)
-                pool_f(k)
-            if ok(k + 1):
-                act_d(k + 1)
-            if ok(k + 3):
-                act_a(k + 3)
-                act_b(k + 3)
-            if W_ON_VECTOR <= wi < PASSES:
-                interleave_weights(W_ORDER[wi], False)
+                vector_xx(k)
+                if k < PIECES - LAST_ON_VECTOR:
+                    product(nc.gpsimd, "i", k, "xx", "v1")
+                    product(nc.gpsimd, "o", k, "t1", "tchn")
+                else:
+                    product(nc.vector, "o", k, "t1", "tchn")
+                    product(nc.vector, "i", k, "xx", "v1")
+            scalar_cycle(k + 1, k + 3, k + 4)
+            if k in w_scalar:
+                interleave_weights(w_scalar[k], False)
             if k >= M_START:
                 done = 0
-                while m_next < PIECES and m_next <= k - 2 and done < 3:
+                while m_next < PIECES and m_next <= k - 1 and done < 3:
                     multiply(m_next)
                     m_next += 1
                     done += 1
             if ok(k + 2):
-                dve_c(k + 2)
-            if ok(k - 1):
-                dve_da_g(k - 1)
-            if ok(k):
-                dve_da_i(k)
-            if ok(k + 3):
-                t_act(k + 3)
-            if ok(k + 1):
-                t_again(k + 1)
+                vector_early(k + 2)
             u = last_piece_of_unit.get(k + 3)
             if u is not None and u + LOAD_BUFS < len(units):
                 load_unit(u + LOAD_BUFS)
+                load_weights(2)

@@ -26,6 +26,7 @@ SPLIT_BLOCKS = 2
 LOAD_BUFS = 4
 W_ORDER = (0, 2, 4, 1, 3, 5)
 W_PARTS = 2
+W_BY_TENSOR = 4
 W_START = 0
 M_START = W_START + 10
 LAST_ON_VECTOR = 2
@@ -113,38 +114,55 @@ def tile_lstmbaseline_pa_v_kernel(tc, x, W_ih0, b_ih0, b_hh0, a_i, a_g, a_o, gra
         grouped_of = {}
         W_COLS = D // W_PARTS
 
-        def interleave_weights(i, on_vector):
-            c, part = W_ORDER[i // W_PARTS], i % W_PARTS
-            grouped = work.tile([P, W_COLS, PACK], BF16, name="grouped", tag="grouped", bufs=4, align_bytes=64)
-            dst = grouped[:].rearrange("p (c i) t -> p c t i", i=4)
-            src = raws[c][:, :, part * W_COLS : (part + 1) * W_COLS].rearrange("p t (c i) -> p c t i", i=4)
-            if on_vector:
-                nc.vector.tensor_copy(out=dst, in_=src)
-            else:
-                nc.scalar.copy(out=dst, in_=src)
-            grouped_of[i] = grouped
+        def grouped_tile(c):
+            grouped = work.tile([P, D, PACK], BF16, name="grouped", tag="grouped", bufs=4, align_bytes=64)
+            grouped_of[c] = grouped
 
-        def quantise_weights(i):
-            c, part = W_ORDER[i // W_PARTS], i % W_PARTS
+        banks = {}
+
+        def tensor_lays_out(c, part):
+            bank = ps_acc.tile([P, W_COLS * PACK], BF16, name="acc")
+            for q in range(2):
+                n0 = part * W_COLS + q * P
+                nc.tensor.matmul(
+                    out=bank[:, q * K_PASS : (q + 1) * K_PASS],
+                    lhsT=ident_bf16[:],
+                    rhs=raws[c][:, :, n0 : n0 + P].rearrange("p t n -> p n t"),
+                    start=True,
+                    stop=True,
+                )
+            banks[c, part] = bank
+
+        def scalar_empties(c, part):
             cols = slice(part * W_COLS, (part + 1) * W_COLS)
-            nc.vector.quantize_mx(
-                out=w_codes[:, c, cols].bitcast(E4M3_X4),
-                scales=w_scales[:, c, cols],
-                in_=grouped_of[i][:].rearrange("p n t -> p (n t)"),
+            nc.scalar.copy(out=grouped_of[c][:, cols, :].rearrange("p n t -> p (n t)"), in_=banks[c, part][:])
+
+        def scalar_lays_out(c, part):
+            cols = slice(part * W_COLS, (part + 1) * W_COLS)
+            nc.scalar.copy(
+                out=grouped_of[c][:, cols, :].rearrange("p (c i) t -> p c t i", i=4),
+                in_=raws[c][:, :, cols].rearrange("p t (c i) -> p c t i", i=4),
             )
 
+        def quantise_weights(c):
+            nc.vector.quantize_mx(
+                out=w_codes[:, c, :].bitcast(E4M3_X4),
+                scales=w_scales[:, c, :],
+                in_=grouped_of[c][:].rearrange("p n t -> p (n t)"),
+            )
+
+        w_tensor = {}
         w_scalar = {}
-        w_vector = {}
         w_quant = {}
-        for i in range(PASSES * W_PARTS):
-            if i % 3 == 2:
-                cyc = W_START + (i // 3) * 2 + 1
-                w_vector[cyc] = i
-                w_quant.setdefault(cyc + 1, []).append(i)
+        for n, c in enumerate(W_ORDER):
+            if n < W_BY_TENSOR:
+                w_tensor[W_START + n] = c
+                w_quant[W_START + n + 2] = c
             else:
-                cyc = W_START + (i // 3) * 2 + i % 3
-                w_scalar[cyc] = i
-                w_quant.setdefault(cyc + 2, []).append(i)
+                first = W_START + W_BY_TENSOR + (n - W_BY_TENSOR) * W_PARTS
+                for part in range(W_PARTS):
+                    w_scalar[first + part] = (c, part)
+                w_quant[first + W_PARTS + 1] = c
 
         S = {}
 
@@ -270,14 +288,16 @@ def tile_lstmbaseline_pa_v_kernel(tc, x, W_ih0, b_ih0, b_hh0, a_i, a_g, a_o, gra
         for k in range(-4, PIECES + 6):
             if ok(k + 3):
                 pe_turn(k + 3)
+            if k in w_tensor:
+                grouped_tile(w_tensor[k])
+                for part in range(W_PARTS):
+                    tensor_lays_out(w_tensor[k], part)
             if ok(k - 1):
                 product(nc.vector, "g", k - 1, "xx", "v2")
                 quantise("o", k - 1)
                 quantise("i", k - 1)
-            if k in w_vector:
-                interleave_weights(w_vector[k], True)
-            for i in w_quant.get(k, []):
-                quantise_weights(i)
+            if k in w_quant:
+                quantise_weights(w_quant[k])
             if ok(k - 1):
                 quantise("g", k - 1)
             if ok(k):
@@ -289,8 +309,13 @@ def tile_lstmbaseline_pa_v_kernel(tc, x, W_ih0, b_ih0, b_hh0, a_i, a_g, a_o, gra
                     product(nc.vector, "o", k, "t1", "tchn")
                     product(nc.vector, "i", k, "xx", "v1")
             scalar_cycle(k + 1, k + 3, k + 4)
+            if k in w_tensor:
+                for part in range(W_PARTS):
+                    scalar_empties(w_tensor[k], part)
             if k in w_scalar:
-                interleave_weights(w_scalar[k], False)
+                if w_scalar[k][1] == 0:
+                    grouped_tile(w_scalar[k][0])
+                scalar_lays_out(w_scalar[k][0], w_scalar[k][1])
             if k >= M_START:
                 done = 0
                 while m_next < PIECES and m_next <= k - 1 and done < 3:

@@ -39,6 +39,10 @@ def flat(tile_ap):
     return tile_ap.rearrange("p w t -> p (w t)")
 
 
+def flat2(tile_ap):
+    return tile_ap.rearrange("p a w t -> p (a w t)")
+
+
 def turned(bank_ap):
     return bank_ap.rearrange("p t w -> p w t")
 
@@ -78,6 +82,9 @@ def tile_lstmbaseline_pa_v_kernel(tc, x, W_ih0, b_ih0, b_hh0, a_i, a_g, a_o, gra
         def wt(name, dtype, bufs):
             return work.tile([P, P, PACK], dtype, name=name, tag=name, bufs=bufs, align_bytes=64)
 
+        def pair(name, dtype, bufs):
+            return work.tile([P, 2, P, PACK], dtype, name=name, tag=name, bufs=bufs, align_bytes=64)
+
         def stt(dst, in0, scalar, in1):
             nc.vector.scalar_tensor_tensor(out=dst, in0=in0, scalar=scalar, in1=in1, op0=ALU.add, op1=ALU.mult)
 
@@ -115,7 +122,7 @@ def tile_lstmbaseline_pa_v_kernel(tc, x, W_ih0, b_ih0, b_hh0, a_i, a_g, a_o, gra
         W_COLS = D // W_PARTS
 
         def grouped_tile(c):
-            grouped = work.tile([P, D, PACK], BF16, name="grouped", tag="grouped", bufs=4, align_bytes=64)
+            grouped = work.tile([P, D, PACK], BF16, name="grouped", tag="grouped", bufs=3, align_bytes=64)
             grouped_of[c] = grouped
 
         banks = {}
@@ -187,16 +194,14 @@ def tile_lstmbaseline_pa_v_kernel(tc, x, W_ih0, b_ih0, b_hh0, a_i, a_g, a_o, gra
 
         def scalar_cycle(jd, jb, ja):
             if ok(jd):
-                tchn = wt("tchn", F32, 3)
-                nc.scalar.activation(out=flat(tchn[:]), in_=flat(S["c", jd][:]), func=FUNC.Tanh, scale=-1.0)
-                S["tchn", jd] = tchn
+                nc.scalar.activation(out=flat(S["right", jd][:, 1]), in_=flat(S["c", jd][:]), func=FUNC.Tanh, scale=-1.0)
             if ok(jb):
                 g_t = wt("g_t", BF16, 3)
                 nc.scalar.copy(out=g_t[:], in_=turned(S["g_ps", jb][:]))
                 S["g_t", jb] = g_t
             if ok(jd):
                 tc2 = wt("tc2", F32, 3)
-                nc.scalar.activation(out=flat(tc2[:]), in_=flat(S["tchn", jd][:]), func=FUNC.Square)
+                nc.scalar.activation(out=flat(tc2[:]), in_=flat(S["right", jd][:, 1]), func=FUNC.Square)
                 S["tc2", jd] = tc2
             if ok(jb):
                 tg = wt("tg", F32, 3)
@@ -204,7 +209,7 @@ def tile_lstmbaseline_pa_v_kernel(tc, x, W_ih0, b_ih0, b_hh0, a_i, a_g, a_o, gra
                 S["tg", jb] = tg
             if ok(ja):
                 tiles, c0 = where[ja]
-                so_n = work.tile([P, K_PASS], F32, name="so_n", tag="so_n", bufs=3)
+                so_n = work.tile([P, K_PASS], F32, name="so_n", tag="so_n", bufs=2)
                 nc.scalar.activation(out=so_n[:], in_=tiles["ao"][:, c0 : c0 + K_PASS], func=FUNC.Sigmoid)
                 S["so_n", ja] = so_n
             if ok(jb):
@@ -224,33 +229,43 @@ def tile_lstmbaseline_pa_v_kernel(tc, x, W_ih0, b_ih0, b_hh0, a_i, a_g, a_o, gra
             nc.vector.tensor_tensor(out=gs[:], in0=so_t, in1=S["g_t", j][:], op=ALU.mult)
             c = wt("c", F32, 3)
             nc.vector.tensor_tensor(out=c[:], in0=si_t, in1=S["tg", j][:], op=ALU.mult)
-            t1 = wt("t1", F32, 4)
-            stt(t1[:], so_t, -1.0, gs[:])
+            left = pair("left", F32, 5)
+            right = pair("right", F32, 4)
+            stt(left[:, 1], so_t, -1.0, gs[:])
             v2 = wt("v2", F32, 5)
             stt(v2[:], S["tg2", j][:], -1.0, si_t)
-            v1 = wt("v1", F32, 4)
-            stt(v1[:], si_t, -1.0, c[:])
+            stt(right[:, 0], si_t, -1.0, c[:])
             S["gs", j] = gs
             S["c", j] = c
-            S["t1", j] = t1
-            S["v1", j] = v1
+            S["left", j] = left
+            S["right", j] = right
             S["v2", j] = v2
 
         def vector_xx(j):
-            xx = wt("xx", F32, 3)
-            stt(flat(xx[:]), flat(S["tc2", j][:]), -1.0, flat(S["gs", j][:]))
-            S["xx", j] = xx
+            stt(flat(S["left", j][:, 0]), flat(S["tc2", j][:]), -1.0, flat(S["gs", j][:]))
 
-        def product(engine, key, j, a, b):
-            da = wt("da_" + key, BF16, 3)
-            engine.tensor_tensor(out=flat(da[:]), in0=flat(S[a, j][:]), in1=flat(S[b, j][:]), op=ALU.mult)
-            S["da_" + key, j] = da
+        def products_io(engine, j):
+            da_io = pair("da_io", BF16, 3)
+            engine.tensor_tensor(out=flat2(da_io[:]), in0=flat2(S["left", j][:]), in1=flat2(S["right", j][:]), op=ALU.mult)
+            S["da_io", j] = da_io
 
-        def quantise(key, j):
-            codes = mxop.tile([P, P], U32, align_bytes=64, name="codes_" + key, tag="codes_" + key)
-            scales = mxop.tile([P, P], U8, align_bytes=64, name="scales_" + key, tag="scales_" + key)
-            nc.vector.quantize_mx(out=codes[:].bitcast(E5M2_X4), scales=scales[:], in_=flat(S["da_" + key, j][:]))
-            S["q_" + key, j] = (codes, scales)
+        def product_g(j):
+            da_g = wt("da_g", BF16, 3)
+            nc.vector.tensor_tensor(out=flat(da_g[:]), in0=flat(S["left", j][:, 0]), in1=flat(S["v2", j][:]), op=ALU.mult)
+            S["da_g", j] = da_g
+
+        def quantise_io(j):
+            codes = mxop.tile([P, 2 * P], U32, align_bytes=64, name="codes_io", tag="codes_io")
+            scales = mxop.tile([P, 2 * P], U8, align_bytes=64, name="scales_io", tag="scales_io")
+            nc.vector.quantize_mx(out=codes[:].bitcast(E5M2_X4), scales=scales[:], in_=flat2(S["da_io", j][:]))
+            S["q_i", j] = (codes[:, 0:P], scales[:, 0:P])
+            S["q_o", j] = (codes[:, P : 2 * P], scales[:, P : 2 * P])
+
+        def quantise_g(j):
+            codes = mxop.tile([P, P], U32, align_bytes=64, name="codes_g", tag="codes_g")
+            scales = mxop.tile([P, P], U8, align_bytes=64, name="scales_g", tag="scales_g")
+            nc.vector.quantize_mx(out=codes[:].bitcast(E5M2_X4), scales=scales[:], in_=flat(S["da_g", j][:]))
+            S["q_g", j] = (codes[:], scales[:])
 
         open_acc = {}
 
@@ -265,8 +280,8 @@ def tile_lstmbaseline_pa_v_kernel(tc, x, W_ih0, b_ih0, b_hh0, a_i, a_g, a_o, gra
                 c = gate * HALVES + h
                 nc.tensor.matmul_mx(
                     out=acc[:],
-                    lhsT=codes[:].bitcast(E5M2_X4),
-                    lhsT_scale=scales[:],
+                    lhsT=codes.bitcast(E5M2_X4),
+                    lhsT_scale=scales,
                     rhs=w_codes[:, c, :].bitcast(E4M3_X4),
                     rhs_scale=w_scales[:, c, :],
                     start=(h == 0 and n == 0),
@@ -293,21 +308,15 @@ def tile_lstmbaseline_pa_v_kernel(tc, x, W_ih0, b_ih0, b_hh0, a_i, a_g, a_o, gra
                 for part in range(W_PARTS):
                     tensor_lays_out(w_tensor[k], part)
             if ok(k - 1):
-                product(nc.vector, "g", k - 1, "xx", "v2")
-                quantise("o", k - 1)
-                quantise("i", k - 1)
+                product_g(k - 1)
+                quantise_io(k - 1)
             if k in w_quant:
                 quantise_weights(w_quant[k])
             if ok(k - 1):
-                quantise("g", k - 1)
+                quantise_g(k - 1)
             if ok(k):
                 vector_xx(k)
-                if k < PIECES - LAST_ON_VECTOR:
-                    product(nc.gpsimd, "i", k, "xx", "v1")
-                    product(nc.gpsimd, "o", k, "t1", "tchn")
-                else:
-                    product(nc.vector, "o", k, "t1", "tchn")
-                    product(nc.vector, "i", k, "xx", "v1")
+                products_io(nc.gpsimd if k < PIECES - LAST_ON_VECTOR else nc.vector, k)
             scalar_cycle(k + 1, k + 3, k + 4)
             if k in w_tensor:
                 for part in range(W_PARTS):

@@ -27,8 +27,10 @@ LOAD_BUFS = 4
 W_ORDER = (0, 2, 4, 1, 3, 5)
 W_PARTS = 2
 W_BY_TENSOR = 4
-W_START = 0
+W_START = 1
 M_START = W_START + 10
+HEAD_SQUARES = 3
+HEAD_COPIES = 3
 LAST_ON_VECTOR = 2
 
 FLOPS = 2 * B * 3 * H * D
@@ -192,13 +194,16 @@ def tile_lstmbaseline_pa_v_kernel(tc, x, W_ih0, b_ih0, b_hh0, a_i, a_g, a_o, gra
             S["so_t", j] = so_t
             S["si_t", j] = si_t
 
+        def copy_g(copy, j):
+            g_t = wt("g_t", BF16, 3)
+            copy(out=g_t[:], in_=turned(S["g_ps", j][:]))
+            S["g_t", j] = g_t
+
         def scalar_cycle(jd, jb, ja):
             if ok(jd):
                 nc.scalar.activation(out=flat(S["right", jd][:, 1]), in_=flat(S["c", jd][:]), func=FUNC.Tanh, scale=-1.0)
-            if ok(jb):
-                g_t = wt("g_t", BF16, 3)
-                nc.scalar.copy(out=g_t[:], in_=turned(S["g_ps", jb][:]))
-                S["g_t", jb] = g_t
+            if ok(jb) and jb >= HEAD_COPIES:
+                copy_g(nc.scalar.copy, jb)
             if ok(jd):
                 tc2 = wt("tc2", F32, 3)
                 nc.scalar.activation(out=flat(tc2[:]), in_=flat(S["right", jd][:, 1]), func=FUNC.Square)
@@ -214,7 +219,10 @@ def tile_lstmbaseline_pa_v_kernel(tc, x, W_ih0, b_ih0, b_hh0, a_i, a_g, a_o, gra
                 S["so_n", ja] = so_n
             if ok(jb):
                 tg2 = wt("tg2", F32, 3)
-                nc.scalar.activation(out=flat(tg2[:]), in_=flat(S["tg", jb][:]), func=FUNC.Square)
+                if jb < HEAD_SQUARES:
+                    nc.gpsimd.tensor_tensor(out=flat(tg2[:]), in0=flat(S["tg", jb][:]), in1=flat(S["tg", jb][:]), op=ALU.mult)
+                else:
+                    nc.scalar.activation(out=flat(tg2[:]), in_=flat(S["tg", jb][:]), func=FUNC.Square)
                 S["tg2", jb] = tg2
             if ok(ja):
                 tiles, c0 = where[ja]
@@ -288,7 +296,7 @@ def tile_lstmbaseline_pa_v_kernel(tc, x, W_ih0, b_ih0, b_hh0, a_i, a_g, a_o, gra
                     stop=(h == HALVES - 1 and n == GATES - 1),
                 )
             if h == HALVES - 1:
-                res = work.tile([P, D], F32, name="res", tag="res", bufs=2)
+                res = work.tile([P, D], F32, name="res", tag="res", bufs=3)
                 nc.scalar.copy(out=res[:], in_=acc[:])
                 nc.sync.dma_start(out=out[r * P : (r + 1) * P, :], in_=res[:])
 
@@ -297,7 +305,7 @@ def tile_lstmbaseline_pa_v_kernel(tc, x, W_ih0, b_ih0, b_hh0, a_i, a_g, a_o, gra
 
         for u in range(LOAD_BUFS):
             load_unit(u)
-        load_weights(2)
+        load_weights(0)
 
         m_next = 0
         for k in range(-4, PIECES + 6):
@@ -333,6 +341,8 @@ def tile_lstmbaseline_pa_v_kernel(tc, x, W_ih0, b_ih0, b_hh0, a_i, a_g, a_o, gra
                     done += 1
             if ok(k + 2):
                 vector_early(k + 2)
+            if 0 <= k + 3 < HEAD_COPIES:
+                copy_g(nc.vector.tensor_copy, k + 3)
             u = last_piece_of_unit.get(k + 3)
             if u is not None and u + LOAD_BUFS < len(units):
                 load_unit(u + LOAD_BUFS)

@@ -31,6 +31,7 @@ W_START = 1
 M_START = W_START + 10
 HEAD_SQUARES = 3
 HEAD_COPIES = 3
+SPLIT_SIGMOIDS = 4
 LAST_ON_VECTOR = 2
 
 FLOPS = 2 * B * 3 * H * D
@@ -98,7 +99,11 @@ def tile_lstmbaseline_pa_v_kernel(tc, x, W_ih0, b_ih0, b_hh0, a_i, a_g, a_o, gra
             rows = slice(r * P, (r + 1) * P)
             cols = slice(h0 * K_PASS, (h0 + nh) * K_PASS)
             tiles = {}
-            for key, src, dtype in (("ao", a_o, F32), ("ai", a_i, F32), ("go", grad_out, BF16), ("ag", a_g, F32)):
+            oi = loads.tile([P, 2, nh * K_PASS], F32, name="ld_oi", tag="ld_oi")
+            nc.sync.dma_start(out=oi[:, 0, :], in_=a_o[rows, cols])
+            nc.sync.dma_start(out=oi[:, 1, :], in_=a_i[rows, cols])
+            tiles["oi"] = oi
+            for key, src, dtype in (("go", grad_out, BF16), ("ag", a_g, F32)):
                 t = loads.tile([P, nh * K_PASS], dtype, name="ld_" + key, tag="ld_" + key)
                 nc.sync.dma_start(out=t[:], in_=src[rows, cols])
                 tiles[key] = t
@@ -186,9 +191,9 @@ def tile_lstmbaseline_pa_v_kernel(tc, x, W_ih0, b_ih0, b_hh0, a_i, a_g, a_o, gra
             ag_t = ps_ag.tile([P, PACK, P], F32, name="ag_t")
             transpose4(ag_t, tiles["ag"], c0, ident_f32)
             so_t = ps_so.tile([P, PACK, P], F32, name="so_t")
-            transpose4(so_t, S["so_n", j], 0, ident_f32)
+            transpose4(so_t, S["sig_n", j][:, 0, :], 0, ident_f32)
             si_t = ps_si.tile([P, PACK, P], F32, name="si_t")
-            transpose4(si_t, S["si_n", j], 0, ident_f32)
+            transpose4(si_t, S["sig_n", j][:, 1, :], 0, ident_f32)
             S["g_ps", j] = g_ps
             S["ag_t", j] = ag_t
             S["so_t", j] = so_t
@@ -214,9 +219,12 @@ def tile_lstmbaseline_pa_v_kernel(tc, x, W_ih0, b_ih0, b_hh0, a_i, a_g, a_o, gra
                 S["tg", jb] = tg
             if ok(ja):
                 tiles, c0 = where[ja]
-                so_n = work.tile([P, K_PASS], F32, name="so_n", tag="so_n", bufs=2)
-                nc.scalar.activation(out=so_n[:], in_=tiles["ao"][:, c0 : c0 + K_PASS], func=FUNC.Sigmoid)
-                S["so_n", ja] = so_n
+                sig_n = work.tile([P, 2, K_PASS], F32, name="sig_n", tag="sig_n", bufs=3)
+                S["sig_n", ja] = sig_n
+                if ja < SPLIT_SIGMOIDS:
+                    nc.scalar.activation(out=sig_n[:, 0, :], in_=tiles["oi"][:, 0, c0 : c0 + K_PASS], func=FUNC.Sigmoid)
+                else:
+                    nc.scalar.activation(out=sig_n[:], in_=tiles["oi"][:, :, c0 : c0 + K_PASS], func=FUNC.Sigmoid)
             if ok(jb):
                 tg2 = wt("tg2", F32, 3)
                 if jb < HEAD_SQUARES:
@@ -226,9 +234,8 @@ def tile_lstmbaseline_pa_v_kernel(tc, x, W_ih0, b_ih0, b_hh0, a_i, a_g, a_o, gra
                 S["tg2", jb] = tg2
             if ok(ja):
                 tiles, c0 = where[ja]
-                si_n = work.tile([P, K_PASS], F32, name="si_n", tag="si_n", bufs=3)
-                nc.scalar.activation(out=si_n[:], in_=tiles["ai"][:, c0 : c0 + K_PASS], func=FUNC.Sigmoid)
-                S["si_n", ja] = si_n
+                if ja < SPLIT_SIGMOIDS:
+                    nc.scalar.activation(out=S["sig_n", ja][:, 1, :], in_=tiles["oi"][:, 1, c0 : c0 + K_PASS], func=FUNC.Sigmoid)
 
         def vector_early(j):
             so_t = turned(S["so_t", j][:])
@@ -315,16 +322,24 @@ def tile_lstmbaseline_pa_v_kernel(tc, x, W_ih0, b_ih0, b_hh0, a_i, a_g, a_o, gra
                 grouped_tile(w_tensor[k])
                 for part in range(W_PARTS):
                     tensor_lays_out(w_tensor[k], part)
-            if ok(k - 1):
+            alone = k >= PIECES - LAST_ON_VECTOR
+            if ok(k - 1) and k - 1 != PIECES - 1:
                 product_g(k - 1)
+            if ok(k) and alone:
+                vector_xx(k)
+            if ok(k - 1):
                 quantise_io(k - 1)
             if k in w_quant:
                 quantise_weights(w_quant[k])
             if ok(k - 1):
                 quantise_g(k - 1)
-            if ok(k):
+            if ok(k) and not alone:
                 vector_xx(k)
-                products_io(nc.gpsimd if k < PIECES - LAST_ON_VECTOR else nc.vector, k)
+                products_io(nc.gpsimd, k)
+            if ok(k) and alone:
+                products_io(nc.vector, k)
+            if k == PIECES - 1:
+                product_g(k)
             scalar_cycle(k + 1, k + 3, k + 4)
             if k in w_tensor:
                 for part in range(W_PARTS):

from contextlib import ExitStack

import concourse.mybir as mybir
from concourse.masks import make_identity

F32 = mybir.dt.float32
BF16 = mybir.dt.bfloat16
U32 = mybir.dt.uint32
U8 = mybir.dt.uint8
E4M3_X4 = mybir.dt.float8_e4m3fn_x4
E5M2_X4 = mybir.dt.float8_e5m2_x4
FUNC = mybir.ActivationFunctionType
ALU = mybir.AluOpType

P = 128
PACK = 4
K_PASS = P * PACK
B, D, H = 1024, 512, 1024
BLOCKS = B // P
HALVES = H // K_PASS
PIECES = BLOCKS * HALVES
GATE_ROW = (0, 2 * H, 3 * H)
GATES = len(GATE_ROW)
PASSES = GATES * HALVES
SPLIT_BLOCKS = 2
LOAD_BUFS = 4
W_ORDER = (0, 2, 4, 1, 3, 5)
W_PARTS = 2
W_BY_TENSOR = 4
W_START = 1
M_START = W_START + 10
HEAD_SQUARES = 3
HEAD_COPIES = 3
SPLIT_SIGMOIDS = 4
LAST_ON_VECTOR = 2

FLOPS = 2 * B * 3 * H * D
BYTES = 3 * B * H * 4 + B * H * 2 + 3 * H * D * 2 + B * D * 4


def flat(tile_ap):
    return tile_ap.rearrange("p w t -> p (w t)")


def flat2(tile_ap):
    return tile_ap.rearrange("p a w t -> p (a w t)")


def turned(bank_ap):
    return bank_ap.rearrange("p t w -> p w t")


def load_units():
    units = []
    for r in range(BLOCKS):
        if r < SPLIT_BLOCKS:
            units.extend([(r, h, 1) for h in range(HALVES)])
        else:
            units.append((r, 0, HALVES))
    return units


def tile_lstmbaseline_pa_v_kernel(tc, x, W_ih0, b_ih0, b_hh0, a_i, a_g, a_o, grad_out, out):
    nc = tc.nc
    with ExitStack() as ctx:
        const = ctx.enter_context(tc.tile_pool(name="const", bufs=1))
        loads = ctx.enter_context(tc.tile_pool(name="loads", bufs=LOAD_BUFS))
        work = ctx.enter_context(tc.tile_pool(name="work", bufs=3))
        mxop = ctx.enter_context(tc.tile_pool(name="mxop", bufs=12))
        wraw = ctx.enter_context(tc.tile_pool(name="wraw", bufs=PASSES))
        ps_ag = ctx.enter_context(tc.psum_pool(name="ps_ag", bufs=1))
        ps_g = ctx.enter_context(tc.psum_pool(name="ps_g", bufs=1))
        ps_so = ctx.enter_context(tc.psum_pool(name="ps_so", bufs=2))
        ps_si = ctx.enter_context(tc.psum_pool(name="ps_si", bufs=2))
        ps_acc = ctx.enter_context(tc.psum_pool(name="ps_acc", bufs=2))
        ctx.enter_context(tc.manual_schedule())

        ident_f32 = const.tile([P, P], F32)
        make_identity(nc, ident_f32[:])
        ident_bf16 = const.tile([P, P], BF16)
        make_identity(nc, ident_bf16[:])
        w_codes = const.tile([P, PASSES, D], U32, align_bytes=64)
        w_scales = const.tile([P, PASSES, D], U8, align_bytes=64)

        def wt(name, dtype, bufs):
            return work.tile([P, P, PACK], dtype, name=name, tag=name, bufs=bufs, align_bytes=64)

        def pair(name, dtype, bufs):
            return work.tile([P, 2, P, PACK], dtype, name=name, tag=name, bufs=bufs, align_bytes=64)

        def stt(dst, in0, scalar, in1):
            nc.vector.scalar_tensor_tensor(out=dst, in0=in0, scalar=scalar, in1=in1, op0=ALU.add, op1=ALU.mult)

        units = load_units()
        where = {}

        def load_unit(u):
            r, h0, nh = units[u]
            rows = slice(r * P, (r + 1) * P)
            cols = slice(h0 * K_PASS, (h0 + nh) * K_PASS)
            tiles = {}
            oi = loads.tile([P, 2, nh * K_PASS], F32, name="ld_oi", tag="ld_oi")
            nc.sync.dma_start(out=oi[:, 0, :], in_=a_o[rows, cols])
            nc.sync.dma_start(out=oi[:, 1, :], in_=a_i[rows, cols])
            tiles["oi"] = oi
            for key, src, dtype in (("go", grad_out, BF16), ("ag", a_g, F32)):
                t = loads.tile([P, nh * K_PASS], dtype, name="ld_" + key, tag="ld_" + key)
                nc.sync.dma_start(out=t[:], in_=src[rows, cols])
                tiles[key] = t
            for h in range(nh):
                where[r * HALVES + h0 + h] = (tiles, h * K_PASS)

        last_piece_of_unit = {(r * HALVES + h0 + nh - 1): u for u, (r, h0, nh) in enumerate(units)}

        raws = {}
        w_to_load = list(W_ORDER)

        def load_weights(count):
            for c in list(w_to_load[:count]):
                row0 = GATE_ROW[c // HALVES] + (c % HALVES) * K_PASS
                raw = wraw.tile([P, PACK, D], BF16, name="wraw", tag="wraw")
                nc.sync.dma_start(
                    out=raw[:], in_=W_ih0[row0 : row0 + K_PASS, :].rearrange("(t p) n -> p t n", p=P)
                )
                raws[c] = raw
                w_to_load.remove(c)

        grouped_of = {}
        W_COLS = D // W_PARTS

        def grouped_tile(c):
            grouped = work.tile([P, D, PACK], BF16, name="grouped", tag="grouped", bufs=3, align_bytes=64)
            grouped_of[c] = grouped

        banks = {}

        def tensor_lays_out(c, part):
            bank = ps_acc.tile([P, W_COLS * PACK], BF16, name="acc")
            for q in range(2):
                n0 = part * W_COLS + q * P
                nc.tensor.matmul(
                    out=bank[:, q * K_PASS : (q + 1) * K_PASS],
                    lhsT=ident_bf16[:],
                    rhs=raws[c][:, :, n0 : n0 + P].rearrange("p t n -> p n t"),
                    start=True,
                    stop=True,
                )
            banks[c, part] = bank

        def scalar_empties(c, part):
            cols = slice(part * W_COLS, (part + 1) * W_COLS)
            nc.scalar.copy(out=grouped_of[c][:, cols, :].rearrange("p n t -> p (n t)"), in_=banks[c, part][:])

        def scalar_lays_out(c, part):
            cols = slice(part * W_COLS, (part + 1) * W_COLS)
            nc.scalar.copy(
                out=grouped_of[c][:, cols, :].rearrange("p (c i) t -> p c t i", i=4),
                in_=raws[c][:, :, cols].rearrange("p t (c i) -> p c t i", i=4),
            )

        def quantise_weights(c):
            nc.vector.quantize_mx(
                out=w_codes[:, c, :].bitcast(E4M3_X4),
                scales=w_scales[:, c, :],
                in_=grouped_of[c][:].rearrange("p n t -> p (n t)"),
            )

        w_tensor = {}
        w_scalar = {}
        w_quant = {}
        for n, c in enumerate(W_ORDER):
            if n < W_BY_TENSOR:
                w_tensor[W_START + n] = c
                w_quant[W_START + n + 2] = c
            else:
                first = W_START + W_BY_TENSOR + (n - W_BY_TENSOR) * W_PARTS
                for part in range(W_PARTS):
                    w_scalar[first + part] = (c, part)
                w_quant[first + W_PARTS + 1] = c

        S = {}

        def transpose4(bank, src, col0, ident):
            for t in range(PACK):
                nc.tensor.transpose(bank[:, t, :], src[:, col0 + t * P : col0 + (t + 1) * P], ident[:])

        def pe_turn(j):
            tiles, c0 = where[j]
            g_ps = ps_g.tile([P, PACK, P], BF16, name="g_ps")
            transpose4(g_ps, tiles["go"], c0, ident_bf16)
            ag_t = ps_ag.tile([P, PACK, P], F32, name="ag_t")
            transpose4(ag_t, tiles["ag"], c0, ident_f32)
            so_t = ps_so.tile([P, PACK, P], F32, name="so_t")
            transpose4(so_t, S["sig_n", j][:, 0, :], 0, ident_f32)
            si_t = ps_si.tile([P, PACK, P], F32, name="si_t")
            transpose4(si_t, S["sig_n", j][:, 1, :], 0, ident_f32)
            S["g_ps", j] = g_ps
            S["ag_t", j] = ag_t
            S["so_t", j] = so_t
            S["si_t", j] = si_t

        def copy_g(copy, j):
            g_t = wt("g_t", BF16, 3)
            copy(out=g_t[:], in_=turned(S["g_ps", j][:]))
            S["g_t", j] = g_t

        def scalar_cycle(jd, jb, ja):
            if ok(jd):
                nc.scalar.activation(out=flat(S["right", jd][:, 1]), in_=flat(S["c", jd][:]), func=FUNC.Tanh, scale=-1.0)
            if ok(jb) and jb >= HEAD_COPIES:
                copy_g(nc.scalar.copy, jb)
            if ok(jd):
                tc2 = wt("tc2", F32, 3)
                nc.scalar.activation(out=flat(tc2[:]), in_=flat(S["right", jd][:, 1]), func=FUNC.Square)
                S["tc2", jd] = tc2
            if ok(jb):
                tg = wt("tg", F32, 3)
                nc.scalar.activation(out=tg[:], in_=turned(S["ag_t", jb][:]), func=FUNC.Tanh)
                S["tg", jb] = tg
            if ok(ja):
                tiles, c0 = where[ja]
                sig_n = work.tile([P, 2, K_PASS], F32, name="sig_n", tag="sig_n", bufs=3)
                S["sig_n", ja] = sig_n
                if ja < SPLIT_SIGMOIDS:
                    nc.scalar.activation(out=sig_n[:, 0, :], in_=tiles["oi"][:, 0, c0 : c0 + K_PASS], func=FUNC.Sigmoid)
                else:
                    nc.scalar.activation(out=sig_n[:], in_=tiles["oi"][:, :, c0 : c0 + K_PASS], func=FUNC.Sigmoid)
            if ok(jb):
                tg2 = wt("tg2", F32, 3)
                if jb < HEAD_SQUARES:
                    nc.gpsimd.tensor_tensor(out=flat(tg2[:]), in0=flat(S["tg", jb][:]), in1=flat(S["tg", jb][:]), op=ALU.mult)
                else:
                    nc.scalar.activation(out=flat(tg2[:]), in_=flat(S["tg", jb][:]), func=FUNC.Square)
                S["tg2", jb] = tg2
            if ok(ja):
                tiles, c0 = where[ja]
                if ja < SPLIT_SIGMOIDS:
                    nc.scalar.activation(out=S["sig_n", ja][:, 1, :], in_=tiles["oi"][:, 1, c0 : c0 + K_PASS], func=FUNC.Sigmoid)

        def vector_early(j):
            so_t = turned(S["so_t", j][:])
            si_t = turned(S["si_t", j][:])
            gs = wt("gs", F32, 4)
            nc.vector.tensor_tensor(out=gs[:], in0=so_t, in1=S["g_t", j][:], op=ALU.mult)
            c = wt("c", F32, 3)
            nc.vector.tensor_tensor(out=c[:], in0=si_t, in1=S["tg", j][:], op=ALU.mult)
            left = pair("left", F32, 5)
            right = pair("right", F32, 4)
            stt(left[:, 1], so_t, -1.0, gs[:])
            v2 = wt("v2", F32, 5)
            stt(v2[:], S["tg2", j][:], -1.0, si_t)
            stt(right[:, 0], si_t, -1.0, c[:])
            S["gs", j] = gs
            S["c", j] = c
            S["left", j] = left
            S["right", j] = right
            S["v2", j] = v2

        def vector_xx(j):
            stt(flat(S["left", j][:, 0]), flat(S["tc2", j][:]), -1.0, flat(S["gs", j][:]))

        def products_io(engine, j):
            da_io = pair("da_io", BF16, 3)
            engine.tensor_tensor(out=flat2(da_io[:]), in0=flat2(S["left", j][:]), in1=flat2(S["right", j][:]), op=ALU.mult)
            S["da_io", j] = da_io

        def product_g(j):
            da_g = wt("da_g", BF16, 3)
            nc.vector.tensor_tensor(out=flat(da_g[:]), in0=flat(S["left", j][:, 0]), in1=flat(S["v2", j][:]), op=ALU.mult)
            S["da_g", j] = da_g

        def quantise_io(j):
            codes = mxop.tile([P, 2 * P], U32, align_bytes=64, name="codes_io", tag="codes_io")
            scales = mxop.tile([P, 2 * P], U8, align_bytes=64, name="scales_io", tag="scales_io")
            nc.vector.quantize_mx(out=codes[:].bitcast(E5M2_X4), scales=scales[:], in_=flat2(S["da_io", j][:]))
            S["q_i", j] = (codes[:, 0:P], scales[:, 0:P])
            S["q_o", j] = (codes[:, P : 2 * P], scales[:, P : 2 * P])

        def quantise_g(j):
            codes = mxop.tile([P, P], U32, align_bytes=64, name="codes_g", tag="codes_g")
            scales = mxop.tile([P, P], U8, align_bytes=64, name="scales_g", tag="scales_g")
            nc.vector.quantize_mx(out=codes[:].bitcast(E5M2_X4), scales=scales[:], in_=flat(S["da_g", j][:]))
            S["q_g", j] = (codes[:], scales[:])

        open_acc = {}

        def multiply(j):
            r, h = divmod(j, HALVES)
            if h == 0:
                acc = ps_acc.tile([P, D], F32, name="acc")
                open_acc[r] = acc
            acc = open_acc[r]
            for n, (key, gate) in enumerate((("o", 2), ("i", 0), ("g", 1))):
                codes, scales = S["q_" + key, j]
                c = gate * HALVES + h
                nc.tensor.matmul_mx(
                    out=acc[:],
                    lhsT=codes.bitcast(E5M2_X4),
                    lhsT_scale=scales,
                    rhs=w_codes[:, c, :].bitcast(E4M3_X4),
                    rhs_scale=w_scales[:, c, :],
                    start=(h == 0 and n == 0),
                    stop=(h == HALVES - 1 and n == GATES - 1),
                )
            if h == HALVES - 1:
                res = work.tile([P, D], F32, name="res", tag="res", bufs=3)
                nc.scalar.copy(out=res[:], in_=acc[:])
                nc.sync.dma_start(out=out[r * P : (r + 1) * P, :], in_=res[:])

        def ok(j):
            return 0 <= j < PIECES

        for u in range(LOAD_BUFS):
            load_unit(u)
        load_weights(0)

        m_next = 0
        for k in range(-4, PIECES + 6):
            if ok(k + 3):
                pe_turn(k + 3)
            if k in w_tensor:
                grouped_tile(w_tensor[k])
                for part in range(W_PARTS):
                    tensor_lays_out(w_tensor[k], part)
            alone = k >= PIECES - LAST_ON_VECTOR
            if ok(k - 1) and k - 1 != PIECES - 1:
                product_g(k - 1)
            if ok(k) and alone:
                vector_xx(k)
            if ok(k - 1):
                quantise_io(k - 1)
            if k in w_quant:
                quantise_weights(w_quant[k])
            if ok(k - 1):
                quantise_g(k - 1)
            if ok(k) and not alone:
                vector_xx(k)
                products_io(nc.gpsimd, k)
            if ok(k) and alone:
                products_io(nc.vector, k)
            if k == PIECES - 1:
                product_g(k)
            scalar_cycle(k + 1, k + 3, k + 4)
            if k in w_tensor:
                for part in range(W_PARTS):
                    scalar_empties(w_tensor[k], part)
            if k in w_scalar:
                if w_scalar[k][1] == 0:
                    grouped_tile(w_scalar[k][0])
                scalar_lays_out(w_scalar[k][0], w_scalar[k][1])
            if k >= M_START:
                done = 0
                while m_next < PIECES and m_next <= k - 1 and done < 3:
                    multiply(m_next)
                    m_next += 1
                    done += 1
            if ok(k + 2):
                vector_early(k + 2)
            if 0 <= k + 3 < HEAD_COPIES:
                copy_g(nc.vector.tensor_copy, k + 3)
            u = last_piece_of_unit.get(k + 3)
            if u is not None and u + LOAD_BUFS < len(units):
                load_unit(u + LOAD_BUFS)
                load_weights(2)
